import numpy as np
import ml_dtypes


def mxq(x, axis, fmt="e4m3"):
    dtype, down = {"e4m3": (ml_dtypes.float8_e4m3fn, 7), "e5m2": (ml_dtypes.float8_e5m2, 14)}[fmt]
    v = np.moveaxis(np.asarray(x, np.float32).astype(ml_dtypes.bfloat16).astype(np.float64), axis, -1)
    blocks = v.reshape(v.shape[:-1] + (-1, 32))
    amax = np.abs(blocks).max(-1, keepdims=True)
    byte = np.maximum(np.where(amax > 0, np.frexp(amax)[1] - 1 + 127, 0) - down, 1)
    scale = np.exp2(byte - 127.0)
    codes = (blocks / scale).astype(np.float32).astype(dtype).astype(np.float64)
    return np.moveaxis((codes * scale).reshape(v.shape), -1, axis)


WIDE = False


def mx_kscale(k):
    if not WIDE:
        return np.ones(k)
    levels = np.array([10, -10, 5, -5, 0])
    a = np.random.permutation(np.resize(levels, k // 512 * 4)).reshape(k // 512, 4)
    idx = np.arange(k)
    return np.exp2(a[idx // 512, idx % 128 // 32])


BF16 = ml_dtypes.bfloat16


def bf(x):
    return np.asarray(x, np.float32).astype(BF16)


def f64(x):
    return np.asarray(x).astype(np.float64)


B, N, D = 4, 1024, 512
EPS = 1e-08


def setup_inputs():
    s = mx_kscale(N)
    x0 = np.random.standard_normal((B, N, D)) / s[None, :, None]
    x1 = np.random.standard_normal((B, N, D))
    sp = np.random.standard_normal((N, N)) / np.sqrt(1.0 + N / D) * s[None, :]
    return {"x": bf(np.concatenate([x0, x1], axis=-1)), "spatial_proj": bf(sp)}


def reference(x, spatial_proj):
    x0, x1 = np.split(f64(x), 2, axis=-1)
    norm = np.sqrt(np.sum(x0 * x0, axis=-1, keepdims=True) + EPS)
    xn = x0 / norm
    xq = mxq(xn, 2, "e4m3")
    cosim = xq @ xq.transpose(0, 2, 1)
    mask = np.tril(f64(spatial_proj))
    attn = mask[None, :, :] * cosim
    ctx = mxq(attn, 2, "e4m3") @ mxq(x0, 1, "e4m3")
    return ctx * x1

@@ -1,0 +1,243 @@
+from contextlib import ExitStack
+
+import concourse.mybir as mybir
+from concourse.masks import make_identity
+
+BF16 = mybir.dt.bfloat16
+F32 = mybir.dt.float32
+U32 = mybir.dt.uint32
+U8 = mybir.dt.uint8
+FP8X4 = mybir.dt.float8_e4m3fn_x4
+ACT = mybir.ActivationFunctionType
+ALU = mybir.AluOpType
+
+B, N, D = 4, 1024, 512
+P = 128
+NT = N // P
+EPS = 1e-08
+FLOPS = 2 * 2 * B * N * N * D
+
+SCALE_ENGINE = {0: "v", 1: "v", 2: "v", 3: "v"}
+REGROUP_ENGINE = {0: "v", 1: "s", 2: "s", 3: "s"}
+
+
+def tile_contextualizer_t_kernel(tc, x, spatial_proj, out):
+    nc = tc.nc
+    with ExitStack() as stack:
+        const = stack.enter_context(tc.tile_pool(name="const", bufs=1))
+        small = stack.enter_context(tc.tile_pool(name="small", bufs=2))
+        xnp = stack.enter_context(tc.tile_pool(name="xnp", bufs=3))
+        gxp = stack.enter_context(tc.tile_pool(name="gxp", bufs=3))
+        xqp = stack.enter_context(tc.tile_pool(name="xqp", bufs=2))
+        g0p = stack.enter_context(tc.tile_pool(name="g0p", bufs=3))
+        x0qp = stack.enter_context(tc.tile_pool(name="x0qp", bufs=2))
+        gap = stack.enter_context(tc.tile_pool(name="gap", bufs=4))
+        aqp = stack.enter_context(tc.tile_pool(name="aqp", bufs=8))
+        outp = stack.enter_context(tc.tile_pool(name="outp", bufs=4))
+        tp = stack.enter_context(tc.psum_pool(name="tp", bufs=2))
+        ps1 = stack.enter_context(tc.psum_pool(name="ps1", bufs=3))
+        ps2 = stack.enter_context(tc.psum_pool(name="ps2", bufs=3))
+
+        xs_in = [const.tile([P, NT, 2 * D], BF16, name="xin%d" % b) for b in range(B)]
+
+        def load_x(b, i0, n):
+            nc.sync.dma_start(
+                out=xs_in[b][:, i0 : i0 + n, :],
+                in_=x[b][i0 * P : (i0 + n) * P, :].rearrange("(i p) c -> p i c", p=P),
+            )
+
+        for c in range(4):
+            load_x(0, 2 * c, 2)
+        spn = const.tile([P, 9 * N], BF16, name="spn")
+        spv = spn[:, 0 : NT * N].rearrange("p (i m) -> p i m", m=N)
+        spd = spn[:, 0 : NT * (N + P)].rearrange("p (i w) -> p i w", w=N + P)[:, :, 0:P]
+        nc.sync.dma_start(
+            out=spv[:, 0:4, 0:512],
+            in_=spatial_proj[0:512, 0:512].rearrange("(i p) m -> p i m", p=P),
+        )
+        nc.sync.dma_start(
+            out=spv[:, 4:8, :],
+            in_=spatial_proj[512:1024, :].rearrange("(i p) m -> p i m", p=P),
+        )
+        for b in range(1, B):
+            load_x(b, 0, 4)
+            load_x(b, 4, 4)
+
+        eps = const.tile([P, 1], F32, name="eps")
+        nc.vector.memset(eps[:], EPS)
+        warm = const.tile([P, 1], F32, name="warm")
+        nc.scalar.activation(out=warm[:], in_=eps[:], func=ACT.Sqrt)
+        ident = const.tile([P, P], BF16, name="ident")
+        make_identity(nc, ident[:])
+        junk = const.tile([P, D], BF16, name="junk")
+        gaz = {}
+        for T in (1, 2, 3):
+            for g in (0, 1):
+                z = const.tile([P, P, 4], BF16, name="gaz%d_%d" % (T, g), align_bytes=64)
+                nc.vector.memset(z[:], 0.0)
+                gaz[(T, g)] = z
+
+        state = [dict() for b in range(B)]
+
+        def prep_chunk(b, c):
+            st = state[b]
+            xin = xs_in[b]
+            if c == 0:
+                st["ss"] = small.tile([P, NT], F32, name="ss")
+                st["nrm"] = small.tile([P, NT], F32, name="nrm")
+                st["rn"] = small.tile([P, NT], F32, name="rn")
+                st["xq"] = xqp.tile([P, N], U32, name="xq", align_bytes=64)
+                st["xs"] = xqp.tile([P, N], U8, name="xs", align_bytes=64)
+                st["x0q"] = x0qp.tile([P, 2, D], U32, name="x0q", align_bytes=64)
+                st["x0s"] = x0qp.tile([P, 2, D], U8, name="x0s", align_bytes=64)
+            if c % 2 == 0:
+                st["gx"] = gxp.tile([P, 4, P, 4], BF16, name="gx", align_bytes=64)
+            i0 = 2 * c
+            for i in (i0, i0 + 1):
+                nc.scalar.activation(
+                    out=junk[:], in_=xin[:, i, 0:D], func=ACT.Square,
+                    accum_out=st["ss"][:, i : i + 1],
+                )
+            nc.scalar.activation(
+                out=st["nrm"][:, i0 : i0 + 2], in_=st["ss"][:, i0 : i0 + 2],
+                func=ACT.Sqrt, bias=eps[:, 0:1],
+            )
+            nc.vector.reciprocal(out=st["rn"][:, i0 : i0 + 2], in_=st["nrm"][:, i0 : i0 + 2])
+            xn = xnp.tile([P, 2, D], BF16, name="xn")
+            for k in range(2):
+                i = i0 + k
+                if SCALE_ENGINE[b] == "v":
+                    nc.vector.tensor_scalar(
+                        out=xn[:, k, :], in0=xin[:, i, 0:D],
+                        scalar1=st["rn"][:, i : i + 1], scalar2=None, op0=ALU.mult,
+                    )
+                else:
+                    nc.scalar.activation(
+                        out=xn[:, k, :], in_=xin[:, i, 0:D], func=ACT.Copy,
+                        scale=st["rn"][:, i : i + 1],
+                    )
+            xt = tp.tile([P, 8, P], BF16, name="xt", tag="tp")
+            for k in range(2):
+                for t in range(4):
+                    nc.tensor.transpose(xt[:, 4 * k + t, :], xn[:, k, t * P : (t + 1) * P], ident[:])
+            k0 = i0 % 4
+            nc.scalar.copy(
+                out=st["gx"][:, k0 : k0 + 2, :, :],
+                in_=xt[:].rearrange("p (k t) r -> p k r t", t=4),
+            )
+            if c % 2 == 1:
+                h = c // 2
+                cols = slice(h * 512, (h + 1) * 512)
+                nc.vector.quantize_mx(
+                    out=st["xq"][:, cols].bitcast(FP8X4),
+                    scales=st["xs"][:, cols],
+                    in_=st["gx"][:].rearrange("p k r t -> p (k r t)"),
+                )
+                g0 = g0p.tile([P, D, 4], BF16, name="g0", align_bytes=64)
+                dst = g0[:].rearrange("p (c i) t -> p c t i", i=4)
+                src = xin[:, 4 * h : 4 * h + 4, 0:D].rearrange("p t (c i) -> p c t i", i=4)
+                if REGROUP_ENGINE[b] == "v":
+                    nc.vector.tensor_copy(out=dst, in_=src)
+                else:
+                    nc.scalar.copy(out=dst, in_=src)
+                nc.vector.quantize_mx(
+                    out=st["x0q"][:, h, :].bitcast(FP8X4),
+                    scales=st["x0s"][:, h, :],
+                    in_=g0[:].rearrange("p d t -> p (d t)"),
+                )
+
+        spg = {}
+        d32 = const.tile([P, NT, P], F32, name="d32")
+
+        def prep_mask(half):
+            rows = range(4 * half, 4 * half + 4)
+            sl = slice(4 * half, 4 * half + 4)
+            nc.vector.tensor_copy(out=d32[:, sl, :], in_=spd[:, sl, :])
+            for i in rows:
+                nc.gpsimd.affine_select(
+                    out=d32[:, i, :], in_=d32[:, i, :], pattern=[[-1, P]],
+                    compare_op=ALU.is_ge, fill=0.0, base=0, channel_multiplier=1,
+                )
+            nc.vector.tensor_copy(out=spd[:, sl, :], in_=d32[:, sl, :])
+            for i in rows:
+                for g in range(i // 4 + 1):
+                    T = min(i - 4 * g, 3) + 1
+                    pst = tp.tile([P, 8, P], BF16, name="pst", tag="tp")
+                    for t in range(T):
+                        j = 4 * g + t
+                        nc.tensor.transpose(pst[:, t, :], spv[:, i, j * P : (j + 1) * P], ident[:])
+                    sg = const.tile([P, P, T], BF16, name="spg%d_%d" % (i, g))
+                    src = pst[:, 0:T, :].rearrange("p t n -> p n t")
+                    if (i + g) % 2 == 0:
+                        nc.vector.tensor_copy(out=sg[:], in_=src)
+                    else:
+                        nc.scalar.copy(out=sg[:], in_=src)
+                    spg[(i, g)] = sg
+
+        def main_tile(b, i):
+            st = state[b]
+            xq, xs = st["xq"], st["xs"]
+            ng = i // 4 + 1
+            ops = []
+            for g in range(ng):
+                T = min(i - 4 * g, 3) + 1
+                c1 = ps1.tile([P, 4, P], F32, name="c1")
+                for t in range(T):
+                    j = 4 * g + t
+                    nc.tensor.matmul_mx(
+                        out=c1[:, t, :],
+                        lhsT=xq[:, j * P : (j + 1) * P].bitcast(FP8X4),
+                        lhsT_scale=xs[:, j * P : (j + 1) * P],
+                        rhs=xq[:, i * P : (i + 1) * P].bitcast(FP8X4),
+                        rhs_scale=xs[:, i * P : (i + 1) * P],
+                        start=True, stop=True,
+                    )
+                if T == 4:
+                    ga = gap.tile([P, P, 4], BF16, name="ga", align_bytes=64)
+                else:
+                    ga = gaz[(T, g)]
+                nc.vector.tensor_tensor(
+                    out=ga[:, :, 0:T],
+                    in0=c1[:, 0:T, :].rearrange("p t n -> p n t"),
+                    in1=spg[(i, g)][:],
+                    op=ALU.mult,
+                )
+                aq = aqp.tile([P, P], U32, name="aq", align_bytes=64)
+                asc = aqp.tile([P, P], U8, name="asc", align_bytes=64)
+                nc.vector.quantize_mx(
+                    out=aq[:].bitcast(FP8X4), scales=asc[:],
+                    in_=ga[:].rearrange("p n t -> p (n t)"),
+                )
+                ops.append((aq, asc))
+            ctxp = ps2.tile([P, D], F32, name="ctxp")
+            for g in range(ng):
+                aq, asc = ops[g]
+                nc.tensor.matmul_mx(
+                    out=ctxp[:],
+                    lhsT=aq[:].bitcast(FP8X4), lhsT_scale=asc[:],
+                    rhs=st["x0q"][:, g, :].bitcast(FP8X4), rhs_scale=st["x0s"][:, g, :],
+                    start=(g == 0), stop=(g == ng - 1),
+                )
+            if i % 2 == 0:
+                st["o"] = outp.tile([P, 2, D], F32, name="o")
+            nc.vector.tensor_tensor(
+                out=st["o"][:, i % 2, :], in0=ctxp[:], in1=xs_in[b][:, i, D : 2 * D], op=ALU.mult,
+            )
+            if i % 2 == 1:
+                nc.sync.dma_start(
+                    out=out[b][(i - 1) * P : (i + 1) * P, :].rearrange("(i p) d -> p i d", p=P),
+                    in_=st["o"][:],
+                )
+
+        prep_chunk(0, 0)
+        prep_chunk(0, 1)
+        prep_mask(0)
+        prep_chunk(0, 2)
+        prep_chunk(0, 3)
+        prep_mask(1)
+        for b in range(B):
+            for c in range(4):
+                main_tile(b, 2 * c)
+                main_tile(b, 2 * c + 1)
+                if b + 1 < B:
+                    prep_chunk(b + 1, c)

@@ -17,8 +17,9 @@ NT = N // P
 EPS = 1e-08
 FLOPS = 2 * 2 * B * N * N * D
 
-SCALE_ENGINE = {0: "v", 1: "v", 2: "v", 3: "v"}
-REGROUP_ENGINE = {0: "v", 1: "s", 2: "s", 3: "s"}
+PIN = True
+NQ = 4 * B
+NS = NT * B
 
 
 def tile_contextualizer_t_kernel(tc, x, spatial_proj, out):
@@ -29,14 +30,15 @@ def tile_contextualizer_t_kernel(tc, x, spatial_proj, out):
         xnp = stack.enter_context(tc.tile_pool(name="xnp", bufs=3))
         gxp = stack.enter_context(tc.tile_pool(name="gxp", bufs=3))
         xqp = stack.enter_context(tc.tile_pool(name="xqp", bufs=2))
-        g0p = stack.enter_context(tc.tile_pool(name="g0p", bufs=3))
+        g0p = stack.enter_context(tc.tile_pool(name="g0p", bufs=2))
         x0qp = stack.enter_context(tc.tile_pool(name="x0qp", bufs=2))
-        gap = stack.enter_context(tc.tile_pool(name="gap", bufs=4))
-        aqp = stack.enter_context(tc.tile_pool(name="aqp", bufs=8))
+        aqp = stack.enter_context(tc.tile_pool(name="aqp", bufs=4))
         outp = stack.enter_context(tc.tile_pool(name="outp", bufs=4))
         tp = stack.enter_context(tc.psum_pool(name="tp", bufs=2))
-        ps1 = stack.enter_context(tc.psum_pool(name="ps1", bufs=3))
-        ps2 = stack.enter_context(tc.psum_pool(name="ps2", bufs=3))
+        ps1 = stack.enter_context(tc.psum_pool(name="ps1", bufs=4))
+        ps2 = stack.enter_context(tc.psum_pool(name="ps2", bufs=2))
+        if PIN:
+            stack.enter_context(tc.manual_schedule())
 
         xs_in = [const.tile([P, NT, 2 * D], BF16, name="xin%d" % b) for b in range(B)]
 
@@ -46,11 +48,19 @@ def tile_contextualizer_t_kernel(tc, x, spatial_proj, out):
                 in_=x[b][i0 * P : (i0 + n) * P, :].rearrange("(i p) c -> p i c", p=P),
             )
 
-        for c in range(4):
-            load_x(0, 2 * c, 2)
         spn = const.tile([P, 9 * N], BF16, name="spn")
         spv = spn[:, 0 : NT * N].rearrange("p (i m) -> p i m", m=N)
         spd = spn[:, 0 : NT * (N + P)].rearrange("p (i w) -> p i w", w=N + P)[:, :, 0:P]
+
+        def load_part(b, i0, n, c0, c1):
+            nc.sync.dma_start(
+                out=xs_in[b][:, i0 : i0 + n, c0:c1],
+                in_=x[b][i0 * P : (i0 + n) * P, c0:c1].rearrange("(i p) c -> p i c", p=P),
+            )
+
+        load_part(0, 0, 2, 0, D)
+        load_part(0, 2, 2, 0, D)
+        load_part(0, 4, 4, 0, D)
         nc.sync.dma_start(
             out=spv[:, 0:4, 0:512],
             in_=spatial_proj[0:512, 0:512].rearrange("(i p) m -> p i m", p=P),
@@ -59,6 +69,7 @@ def tile_contextualizer_t_kernel(tc, x, spatial_proj, out):
             out=spv[:, 4:8, :],
             in_=spatial_proj[512:1024, :].rearrange("(i p) m -> p i m", p=P),
         )
+        load_part(0, 0, 8, D, 2 * D)
         for b in range(1, B):
             load_x(b, 0, 4)
             load_x(b, 4, 4)
@@ -70,118 +81,165 @@ def tile_contextualizer_t_kernel(tc, x, spatial_proj, out):
         ident = const.tile([P, P], BF16, name="ident")
         make_identity(nc, ident[:])
         junk = const.tile([P, D], BF16, name="junk")
-        gaz = {}
-        for T in (1, 2, 3):
-            for g in (0, 1):
-                z = const.tile([P, P, 4], BF16, name="gaz%d_%d" % (T, g), align_bytes=64)
-                nc.vector.memset(z[:], 0.0)
-                gaz[(T, g)] = z
+        ga_t = {}
+        for par in range(2):
+            for i in range(NT):
+                ng = i // 4 + 1
+                z = const.tile([P, ng, P, 4], BF16, name="ga%d_%d" % (i, par), align_bytes=64)
+                if i % 4 != 3:
+                    nc.vector.memset(z[:, ng - 1, :, :], 0.0)
+                ga_t[(i, par)] = z
 
         state = [dict() for b in range(B)]
+        chunk = [dict() for q in range(NQ)]
+        tl = [dict() for s in range(NS)]
 
-        def prep_chunk(b, c):
+        def s_sumsq(q):
+            if not 0 <= q < NQ:
+                return
+            b, c = q // 4, q % 4
             st = state[b]
-            xin = xs_in[b]
             if c == 0:
                 st["ss"] = small.tile([P, NT], F32, name="ss")
                 st["nrm"] = small.tile([P, NT], F32, name="nrm")
                 st["rn"] = small.tile([P, NT], F32, name="rn")
-                st["xq"] = xqp.tile([P, N], U32, name="xq", align_bytes=64)
-                st["xs"] = xqp.tile([P, N], U8, name="xs", align_bytes=64)
-                st["x0q"] = x0qp.tile([P, 2, D], U32, name="x0q", align_bytes=64)
-                st["x0s"] = x0qp.tile([P, 2, D], U8, name="x0s", align_bytes=64)
-            if c % 2 == 0:
-                st["gx"] = gxp.tile([P, 4, P, 4], BF16, name="gx", align_bytes=64)
             i0 = 2 * c
             for i in (i0, i0 + 1):
                 nc.scalar.activation(
-                    out=junk[:], in_=xin[:, i, 0:D], func=ACT.Square,
+                    out=junk[:], in_=xs_in[b][:, i, 0:D], func=ACT.Square,
                     accum_out=st["ss"][:, i : i + 1],
                 )
             nc.scalar.activation(
                 out=st["nrm"][:, i0 : i0 + 2], in_=st["ss"][:, i0 : i0 + 2],
                 func=ACT.Sqrt, bias=eps[:, 0:1],
             )
-            nc.vector.reciprocal(out=st["rn"][:, i0 : i0 + 2], in_=st["nrm"][:, i0 : i0 + 2])
+
+        def v_recip(q):
+            if not 0 <= q < NQ:
+                return
+            b, c = q // 4, q % 4
+            st = state[b]
+            nc.vector.reciprocal(out=st["rn"][:, 2 * c : 2 * c + 2], in_=st["nrm"][:, 2 * c : 2 * c + 2])
+
+        def v_scale(q):
+            if not 0 <= q < NQ:
+                return
+            b, c = q // 4, q % 4
+            st = state[b]
             xn = xnp.tile([P, 2, D], BF16, name="xn")
+            chunk[q]["xn"] = xn
             for k in range(2):
-                i = i0 + k
-                if SCALE_ENGINE[b] == "v":
-                    nc.vector.tensor_scalar(
-                        out=xn[:, k, :], in0=xin[:, i, 0:D],
-                        scalar1=st["rn"][:, i : i + 1], scalar2=None, op0=ALU.mult,
-                    )
-                else:
-                    nc.scalar.activation(
-                        out=xn[:, k, :], in_=xin[:, i, 0:D], func=ACT.Copy,
-                        scale=st["rn"][:, i : i + 1],
-                    )
-            xt = tp.tile([P, 8, P], BF16, name="xt", tag="tp")
+                i = 2 * c + k
+                nc.vector.tensor_scalar(
+                    out=xn[:, k, :], in0=xs_in[b][:, i, 0:D],
+                    scalar1=st["rn"][:, i : i + 1], scalar2=None, op0=ALU.mult,
+                )
+
+        def pe_transpose(q):
+            if not 0 <= q < NQ:
+                return
+            xn = chunk[q]["xn"]
+            xt = tp.tile([P, 8, P], BF16, name="xt")
+            chunk[q]["xt"] = xt
             for k in range(2):
                 for t in range(4):
                     nc.tensor.transpose(xt[:, 4 * k + t, :], xn[:, k, t * P : (t + 1) * P], ident[:])
-            k0 = i0 % 4
-            nc.scalar.copy(
-                out=st["gx"][:, k0 : k0 + 2, :, :],
-                in_=xt[:].rearrange("p (k t) r -> p k r t", t=4),
+
+        def s_evac(q):
+            if not 0 <= q < NQ:
+                return
+            gx = gxp.tile([P, 2, P, 4], BF16, name="gx", align_bytes=64)
+            chunk[q]["gx"] = gx
+            nc.scalar.copy(out=gx[:], in_=chunk[q]["xt"][:].rearrange("p (k t) r -> p k r t", t=4))
+
+        def v_quant_xn(q):
+            if not 0 <= q < NQ:
+                return
+            b, c = q // 4, q % 4
+            st = state[b]
+            if c == 0:
+                st["xq"] = xqp.tile([P, N], U32, name="xq", align_bytes=64)
+                st["xs"] = xqp.tile([P, N], U8, name="xs", align_bytes=64)
+            cols = slice(c * 256, (c + 1) * 256)
+            nc.vector.quantize_mx(
+                out=st["xq"][:, cols].bitcast(FP8X4), scales=st["xs"][:, cols],
+                in_=chunk[q]["gx"][:].rearrange("p k r t -> p (k r t)"),
             )
-            if c % 2 == 1:
-                h = c // 2
-                cols = slice(h * 512, (h + 1) * 512)
-                nc.vector.quantize_mx(
-                    out=st["xq"][:, cols].bitcast(FP8X4),
-                    scales=st["xs"][:, cols],
-                    in_=st["gx"][:].rearrange("p k r t -> p (k r t)"),
-                )
-                g0 = g0p.tile([P, D, 4], BF16, name="g0", align_bytes=64)
-                dst = g0[:].rearrange("p (c i) t -> p c t i", i=4)
-                src = xin[:, 4 * h : 4 * h + 4, 0:D].rearrange("p t (c i) -> p c t i", i=4)
-                if REGROUP_ENGINE[b] == "v":
-                    nc.vector.tensor_copy(out=dst, in_=src)
-                else:
-                    nc.scalar.copy(out=dst, in_=src)
-                nc.vector.quantize_mx(
-                    out=st["x0q"][:, h, :].bitcast(FP8X4),
-                    scales=st["x0s"][:, h, :],
-                    in_=g0[:].rearrange("p d t -> p (d t)"),
-                )
+
+        def regroup(eng, b, g, d0, d1):
+            st = state[b]
+            if d0 == 0:
+                st["g0_%d" % g] = g0p.tile([P, D, 4], BF16, name="g0", align_bytes=64)
+            g0 = st["g0_%d" % g]
+            dst = g0[:, d0:d1, :].rearrange("p (c i) t -> p c t i", i=4)
+            src = xs_in[b][:, 4 * g : 4 * g + 4, d0:d1].rearrange("p t (c i) -> p c t i", i=4)
+            if eng == "v":
+                nc.vector.tensor_copy(out=dst, in_=src)
+            else:
+                nc.scalar.copy(out=dst, in_=src)
+
+        def s_regroup(q):
+            if not 4 <= q < NQ:
+                return
+            b, c = q // 4, q % 4
+            regroup("s", b, c // 2, (c % 2) * 256, (c % 2) * 256 + 256)
+
+        def v_quant_x0(b, g):
+            if not 0 <= b < B:
+                return
+            st = state[b]
+            if g == 0:
+                st["x0q"] = x0qp.tile([P, 2, D], U32, name="x0q", align_bytes=64)
+                st["x0s"] = x0qp.tile([P, 2, D], U8, name="x0s", align_bytes=64)
+            nc.vector.quantize_mx(
+                out=st["x0q"][:, g, :].bitcast(FP8X4), scales=st["x0s"][:, g, :],
+                in_=st["g0_%d" % g][:].rearrange("p d t -> p (d t)"),
+            )
 
         spg = {}
+        pst_t = {}
         d32 = const.tile([P, NT, P], F32, name="d32")
 
-        def prep_mask(half):
-            rows = range(4 * half, 4 * half + 4)
+        def mask_a(half):
             sl = slice(4 * half, 4 * half + 4)
             nc.vector.tensor_copy(out=d32[:, sl, :], in_=spd[:, sl, :])
-            for i in rows:
+            for i in range(4 * half, 4 * half + 4):
                 nc.gpsimd.affine_select(
                     out=d32[:, i, :], in_=d32[:, i, :], pattern=[[-1, P]],
                     compare_op=ALU.is_ge, fill=0.0, base=0, channel_multiplier=1,
                 )
-            nc.vector.tensor_copy(out=spd[:, sl, :], in_=d32[:, sl, :])
-            for i in rows:
-                for g in range(i // 4 + 1):
-                    T = min(i - 4 * g, 3) + 1
-                    pst = tp.tile([P, 8, P], BF16, name="pst", tag="tp")
-                    for t in range(T):
-                        j = 4 * g + t
-                        nc.tensor.transpose(pst[:, t, :], spv[:, i, j * P : (j + 1) * P], ident[:])
-                    sg = const.tile([P, P, T], BF16, name="spg%d_%d" % (i, g))
-                    src = pst[:, 0:T, :].rearrange("p t n -> p n t")
-                    if (i + g) % 2 == 0:
-                        nc.vector.tensor_copy(out=sg[:], in_=src)
-                    else:
-                        nc.scalar.copy(out=sg[:], in_=src)
-                    spg[(i, g)] = sg
 
-        def main_tile(b, i):
-            st = state[b]
-            xq, xs = st["xq"], st["xs"]
-            ng = i // 4 + 1
-            ops = []
-            for g in range(ng):
+        def mask_b(half):
+            sl = slice(4 * half, 4 * half + 4)
+            nc.vector.tensor_copy(out=spd[:, sl, :], in_=d32[:, sl, :])
+
+        def mask_t(i):
+            pst = ps1.tile([P, 8, P], BF16, name="pst", tag="c1")
+            pst_t[i] = pst
+            for j in range(i + 1):
+                nc.tensor.transpose(pst[:, j, :], spv[:, i, j * P : (j + 1) * P], ident[:])
+
+        def mask_e(i):
+            for g in range(i // 4 + 1):
                 T = min(i - 4 * g, 3) + 1
-                c1 = ps1.tile([P, 4, P], F32, name="c1")
+                sg = const.tile([P, P, T], BF16, name="spg%d_%d" % (i, g))
+                src = pst_t[i][:, 4 * g : 4 * g + T, :].rearrange("p t n -> p n t")
+                if i >= 4:
+                    nc.scalar.copy(out=sg[:], in_=src)
+                else:
+                    nc.vector.tensor_copy(out=sg[:], in_=src)
+                spg[(i, g)] = sg
+
+        def pe_cosim(s):
+            if not 0 <= s < NS:
+                return
+            b, i = s // NT, s % NT
+            xq, xs = state[b]["xq"], state[b]["xs"]
+            tl[s]["c1"] = []
+            for g in range(i // 4 + 1):
+                T = min(i - 4 * g, 3) + 1
+                c1 = ps1.tile([P, 4, P], F32, name="c1", tag="c1")
+                tl[s]["c1"].append(c1)
                 for t in range(T):
                     j = 4 * g + t
                     nc.tensor.matmul_mx(
@@ -192,52 +250,142 @@ def tile_contextualizer_t_kernel(tc, x, spatial_proj, out):
                         rhs_scale=xs[:, i * P : (i + 1) * P],
                         start=True, stop=True,
                     )
-                if T == 4:
-                    ga = gap.tile([P, P, 4], BF16, name="ga", align_bytes=64)
-                else:
-                    ga = gaz[(T, g)]
+
+        def v_mask(s):
+            if not 0 <= s < NS:
+                return
+            b, i = s // NT, s % NT
+            ga = ga_t[(i, b % 2)]
+            for g in range(i // 4 + 1):
+                T = min(i - 4 * g, 3) + 1
                 nc.vector.tensor_tensor(
-                    out=ga[:, :, 0:T],
-                    in0=c1[:, 0:T, :].rearrange("p t n -> p n t"),
+                    out=ga[:, g, :, 0:T],
+                    in0=tl[s]["c1"][g][:, 0:T, :].rearrange("p t n -> p n t"),
                     in1=spg[(i, g)][:],
                     op=ALU.mult,
                 )
-                aq = aqp.tile([P, P], U32, name="aq", align_bytes=64)
-                asc = aqp.tile([P, P], U8, name="asc", align_bytes=64)
-                nc.vector.quantize_mx(
-                    out=aq[:].bitcast(FP8X4), scales=asc[:],
-                    in_=ga[:].rearrange("p n t -> p (n t)"),
-                )
-                ops.append((aq, asc))
+
+        def v_quant_attn(s):
+            if not 0 <= s < NS:
+                return
+            b, i = s // NT, s % NT
+            ng = i // 4 + 1
+            aq = aqp.tile([P, 2, P], U32, name="aq", align_bytes=64)
+            asc = aqp.tile([P, 2, P], U8, name="asc", align_bytes=64)
+            tl[s]["aq"], tl[s]["asc"] = aq, asc
+            nc.vector.quantize_mx(
+                out=aq[:, 0:ng, :].rearrange("p g n -> p (g n)").bitcast(FP8X4),
+                scales=asc[:, 0:ng, :].rearrange("p g n -> p (g n)"),
+                in_=ga_t[(i, b % 2)][:].rearrange("p g n t -> p (g n t)"),
+            )
+
+        def pe_ctx(s):
+            if not 0 <= s < NS:
+                return
+            b, i = s // NT, s % NT
+            st = state[b]
+            ng = i // 4 + 1
             ctxp = ps2.tile([P, D], F32, name="ctxp")
+            tl[s]["ctx"] = ctxp
             for g in range(ng):
-                aq, asc = ops[g]
                 nc.tensor.matmul_mx(
                     out=ctxp[:],
-                    lhsT=aq[:].bitcast(FP8X4), lhsT_scale=asc[:],
+                    lhsT=tl[s]["aq"][:, g, :].bitcast(FP8X4), lhsT_scale=tl[s]["asc"][:, g, :],
                     rhs=st["x0q"][:, g, :].bitcast(FP8X4), rhs_scale=st["x0s"][:, g, :],
                     start=(g == 0), stop=(g == ng - 1),
                 )
+
+        def v_gate(s):
+            if not 0 <= s < NS:
+                return
+            b, i = s // NT, s % NT
+            st = state[b]
             if i % 2 == 0:
                 st["o"] = outp.tile([P, 2, D], F32, name="o")
+            o = st["o"]
             nc.vector.tensor_tensor(
-                out=st["o"][:, i % 2, :], in0=ctxp[:], in1=xs_in[b][:, i, D : 2 * D], op=ALU.mult,
+                out=o[:, i % 2, :], in0=tl[s]["ctx"][:], in1=xs_in[b][:, i, D : 2 * D], op=ALU.mult,
             )
-            if i % 2 == 1:
+            if s >= NS - 2:
+                nc.sync.dma_start(out=out[b][i * P : (i + 1) * P, :], in_=o[:, i % 2, :])
+            elif i % 2 == 1:
                 nc.sync.dma_start(
                     out=out[b][(i - 1) * P : (i + 1) * P, :].rearrange("(i p) d -> p i d", p=P),
-                    in_=st["o"][:],
+                    in_=o[:],
                 )
 
-        prep_chunk(0, 0)
-        prep_chunk(0, 1)
-        prep_mask(0)
-        prep_chunk(0, 2)
-        prep_chunk(0, 3)
-        prep_mask(1)
-        for b in range(B):
-            for c in range(4):
-                main_tile(b, 2 * c)
-                main_tile(b, 2 * c + 1)
-                if b + 1 < B:
-                    prep_chunk(b + 1, c)
+        s_sumsq(0)
+        regroup("v", 0, 0, 0, D)
+        v_recip(0)
+        v_scale(0)
+        pe_transpose(0)
+
+        s_sumsq(1)
+        v_quant_x0(0, 0)
+        v_recip(1)
+        v_scale(1)
+        pe_transpose(1)
+        mask_a(0)
+
+        s_evac(0)
+        s_sumsq(2)
+        regroup("v", 0, 1, 0, D)
+        mask_a(1)
+        mask_b(0)
+        for i in range(4):
+            mask_t(i)
+        v_quant_xn(0)
+        v_recip(2)
+        mask_e(0)
+        pe_cosim(0)
+        v_scale(2)
+        mask_e(1)
+        pe_cosim(1)
+        pe_transpose(2)
+        mask_b(1)
+        v_quant_x0(0, 1)
+
+        s_evac(1)
+        mask_e(2)
+        mask_t(4)
+        v_mask(0)
+        mask_e(3)
+        mask_t(5)
+        v_quant_xn(1)
+
+        for k in range(0, NQ + 1):
+            q = k + 3
+            s_sumsq(q)
+            s_evac(q - 1)
+            s_regroup(q)
+            if k == 0:
+                mask_e(4)
+                mask_e(5)
+
+            s = 2 * k
+            v_mask(s + 1)
+            v_quant_attn(s)
+            if k == 0:
+                pe_cosim(s + 2)
+            pe_ctx(s)
+            v_gate(s - 1)
+            if k == 0:
+                mask_t(6)
+                mask_t(7)
+
+            s = 2 * k + 1
+            v_mask(s + 1)
+            v_quant_attn(s)
+            pe_cosim(s + 2)
+            pe_ctx(s)
+            v_recip(q)
+            v_gate(s - 1)
+            if (q - 1) % 2 == 1 and q - 1 >= 4:
+                v_quant_x0((q - 1) // 4, ((q - 1) % 4) // 2)
+            v_quant_xn(q - 1)
+            if k == 0:
+                mask_e(6)
+                mask_e(7)
+            pe_cosim(s + 3)
+            v_scale(q)
+            pe_transpose(q)

@@ -7,6 +7,7 @@ BF16 = mybir.dt.bfloat16
 F32 = mybir.dt.float32
 U32 = mybir.dt.uint32
 U8 = mybir.dt.uint8
+I32 = mybir.dt.int32
 FP8X4 = mybir.dt.float8_e4m3fn_x4
 ACT = mybir.ActivationFunctionType
 ALU = mybir.AluOpType
@@ -81,14 +82,18 @@ def tile_contextualizer_t_kernel(tc, x, spatial_proj, out):
         ident = const.tile([P, P], BF16, name="ident")
         make_identity(nc, ident[:])
         junk = const.tile([P, D], BF16, name="junk")
-        ga_t = {}
-        for par in range(2):
-            for i in range(NT):
-                ng = i // 4 + 1
-                z = const.tile([P, ng, P, 4], BF16, name="ga%d_%d" % (i, par), align_bytes=64)
-                if i % 4 != 3:
-                    nc.vector.memset(z[:, ng - 1, :, :], 0.0)
-                ga_t[(i, par)] = z
+        ga_all = const.tile([P, 2, 12, 4 * P], BF16, name="ga_all", align_bytes=64)
+        ga_i32 = (
+            ga_all[:].rearrange("p a u c -> p (a u c)").bitcast(I32)
+            .rearrange("p (a u w) -> p a u w", a=2, u=12)
+        )
+        nc.vector.memset(ga_i32[:, :, 0:3, :], 0)
+        nc.vector.memset(
+            ga_i32[:, :, 4:12, :].rearrange("p a (i g) w -> p a i g w", g=2)[:, :, 0:3, 1, :], 0
+        )
+
+        def unit0(i):
+            return i if i < 4 else 4 + 2 * (i - 4)
 
         state = [dict() for b in range(B)]
         chunk = [dict() for q in range(NQ)]
@@ -213,8 +218,11 @@ def tile_contextualizer_t_kernel(tc, x, spatial_proj, out):
             sl = slice(4 * half, 4 * half + 4)
             nc.vector.tensor_copy(out=spd[:, sl, :], in_=d32[:, sl, :])
 
-        def mask_t(i):
-            pst = ps1.tile([P, 8, P], BF16, name="pst", tag="c1")
+        def mask_t(i, in_ctx_banks=False):
+            if in_ctx_banks:
+                pst = ps2.tile([P, 8, P], BF16, name="pst2", tag="ctxp")
+            else:
+                pst = ps1.tile([P, 8, P], BF16, name="pst", tag="c1")
             pst_t[i] = pst
             for j in range(i + 1):
                 nc.tensor.transpose(pst[:, j, :], spv[:, i, j * P : (j + 1) * P], ident[:])
@@ -255,11 +263,11 @@ def tile_contextualizer_t_kernel(tc, x, spatial_proj, out):
             if not 0 <= s < NS:
                 return
             b, i = s // NT, s % NT
-            ga = ga_t[(i, b % 2)]
             for g in range(i // 4 + 1):
                 T = min(i - 4 * g, 3) + 1
+                ga = ga_all[:, b % 2, unit0(i) + g, :].rearrange("p (n t) -> p n t", t=4)
                 nc.vector.tensor_tensor(
-                    out=ga[:, g, :, 0:T],
+                    out=ga[:, :, 0:T],
                     in0=tl[s]["c1"][g][:, 0:T, :].rearrange("p t n -> p n t"),
                     in1=spg[(i, g)][:],
                     op=ALU.mult,
@@ -276,7 +284,7 @@ def tile_contextualizer_t_kernel(tc, x, spatial_proj, out):
             nc.vector.quantize_mx(
                 out=aq[:, 0:ng, :].rearrange("p g n -> p (g n)").bitcast(FP8X4),
                 scales=asc[:, 0:ng, :].rearrange("p g n -> p (g n)"),
-                in_=ga_t[(i, b % 2)][:].rearrange("p g n t -> p (g n t)"),
+                in_=ga_all[:, b % 2, unit0(i) : unit0(i) + ng, :].rearrange("p u c -> p (u c)"),
             )
 
         def pe_ctx(s):
@@ -285,7 +293,7 @@ def tile_contextualizer_t_kernel(tc, x, spatial_proj, out):
             b, i = s // NT, s % NT
             st = state[b]
             ng = i // 4 + 1
-            ctxp = ps2.tile([P, D], F32, name="ctxp")
+            ctxp = ps2.tile([P, D], F32, name="ctxp", tag="ctxp")
             tl[s]["ctx"] = ctxp
             for g in range(ng):
                 nc.tensor.matmul_mx(
@@ -314,78 +322,93 @@ def tile_contextualizer_t_kernel(tc, x, spatial_proj, out):
                     in_=o[:],
                 )
 
+        H2 = D // 2
         s_sumsq(0)
-        regroup("v", 0, 0, 0, D)
+        regroup("v", 0, 0, 0, H2)
         v_recip(0)
         v_scale(0)
         pe_transpose(0)
 
         s_sumsq(1)
-        v_quant_x0(0, 0)
+        regroup("v", 0, 0, H2, D)
         v_recip(1)
         v_scale(1)
         pe_transpose(1)
         mask_a(0)
+        v_quant_x0(0, 0)
 
         s_evac(0)
         s_sumsq(2)
-        regroup("v", 0, 1, 0, D)
         mask_a(1)
+        v_quant_xn(0)
+        regroup("v", 0, 1, 0, H2)
+        v_recip(2)
+        v_scale(2)
+        pe_transpose(2)
+        regroup("v", 0, 1, H2, D)
         mask_b(0)
         for i in range(4):
             mask_t(i)
-        v_quant_xn(0)
-        v_recip(2)
-        mask_e(0)
-        pe_cosim(0)
-        v_scale(2)
-        mask_e(1)
-        pe_cosim(1)
-        pe_transpose(2)
-        mask_b(1)
-        v_quant_x0(0, 1)
 
         s_evac(1)
-        mask_e(2)
-        mask_t(4)
-        v_mask(0)
-        mask_e(3)
-        mask_t(5)
+        s_sumsq(3)
         v_quant_xn(1)
+        mask_b(1)
+        mask_t(4, True)
+        mask_t(5, True)
+        v_quant_x0(0, 1)
+        v_recip(3)
+        v_scale(3)
+        pe_transpose(3)
+        for i in range(4):
+            mask_e(i)
+        for s in range(4):
+            pe_cosim(s)
 
-        for k in range(0, NQ + 1):
-            q = k + 3
+        s_evac(2)
+        mask_e(4)
+        mask_e(5)
+        v_quant_xn(2)
+        v_mask(0)
+        v_mask(1)
+        mask_t(6)
+        mask_t(7)
+        v_quant_attn(0)
+        v_quant_attn(1)
+        pe_ctx(0)
+        pe_ctx(1)
+        s_evac(3)
+
+        for k in range(NQ):
+            q = k + 4
             s_sumsq(q)
-            s_evac(q - 1)
+            if k > 0:
+                s_evac(q - 1)
             s_regroup(q)
-            if k == 0:
-                mask_e(4)
-                mask_e(5)
-
-            s = 2 * k
-            v_mask(s + 1)
-            v_quant_attn(s)
-            if k == 0:
-                pe_cosim(s + 2)
-            pe_ctx(s)
-            v_gate(s - 1)
-            if k == 0:
-                mask_t(6)
-                mask_t(7)
-
-            s = 2 * k + 1
-            v_mask(s + 1)
-            v_quant_attn(s)
-            pe_cosim(s + 2)
-            pe_ctx(s)
-            v_recip(q)
-            v_gate(s - 1)
-            if (q - 1) % 2 == 1 and q - 1 >= 4:
-                v_quant_x0((q - 1) // 4, ((q - 1) % 4) // 2)
-            v_quant_xn(q - 1)
             if k == 0:
                 mask_e(6)
                 mask_e(7)
-            pe_cosim(s + 3)
+            v_mask(2 * k + 2)
+            v_mask(2 * k + 3)
+            pe_cosim(2 * k + 4)
+            pe_cosim(2 * k + 5)
+            if k != NQ - 2:
+                v_gate(2 * k)
+                v_gate(2 * k + 1)
+                v_recip(q)
+                v_quant_attn(2 * k + 2)
+                v_quant_attn(2 * k + 3)
+                pe_ctx(2 * k + 2)
+                pe_ctx(2 * k + 3)
+            else:
+                v_gate(2 * k)
+                v_quant_attn(2 * k + 2)
+                pe_ctx(2 * k + 2)
+                v_gate(2 * k + 1)
+                v_quant_attn(2 * k + 3)
+                pe_ctx(2 * k + 3)
+            if (q - 1) % 2 == 1 and q - 1 >= 4:
+                v_quant_x0((q - 1) // 4, ((q - 1) % 4) // 2)
             v_scale(q)
             pe_transpose(q)
+            v_quant_xn(q - 1)

@@ -41,7 +41,11 @@ def tile_contextualizer_t_kernel(tc, x, spatial_proj, out):
         if PIN:
             stack.enter_context(tc.manual_schedule())
 
-        xs_in = [const.tile([P, NT, 2 * D], BF16, name="xin%d" % b) for b in range(B)]
+        x0_first = const.tile([P, NT, D], BF16, name="x0_first")
+        x1_first = const.tile([P, NT, D], BF16, name="x1_first")
+        xs_in = [None] + [const.tile([P, NT, 2 * D], BF16, name="xin%d" % b) for b in range(1, B)]
+        x0_sb = [x0_first[:]] + [xs_in[b][:, :, 0:D] for b in range(1, B)]
+        x1_sb = [x1_first[:]] + [xs_in[b][:, :, D : 2 * D] for b in range(1, B)]
 
         def load_x(b, i0, n):
             nc.sync.dma_start(
@@ -53,15 +57,15 @@ def tile_contextualizer_t_kernel(tc, x, spatial_proj, out):
         spv = spn[:, 0 : NT * N].rearrange("p (i m) -> p i m", m=N)
         spd = spn[:, 0 : NT * (N + P)].rearrange("p (i w) -> p i w", w=N + P)[:, :, 0:P]
 
-        def load_part(b, i0, n, c0, c1):
+        def load_first(dst, i0, n, c0):
             nc.sync.dma_start(
-                out=xs_in[b][:, i0 : i0 + n, c0:c1],
-                in_=x[b][i0 * P : (i0 + n) * P, c0:c1].rearrange("(i p) c -> p i c", p=P),
+                out=dst[:, i0 : i0 + n, :],
+                in_=x[0][i0 * P : (i0 + n) * P, c0 : c0 + D].rearrange("(i p) c -> p i c", p=P),
             )
 
-        load_part(0, 0, 2, 0, D)
-        load_part(0, 2, 2, 0, D)
-        load_part(0, 4, 4, 0, D)
+        load_first(x0_first, 0, 2, 0)
+        load_first(x0_first, 2, 2, 0)
+        load_first(x0_first, 4, 4, 0)
         nc.sync.dma_start(
             out=spv[:, 0:4, 0:512],
             in_=spatial_proj[0:512, 0:512].rearrange("(i p) m -> p i m", p=P),
@@ -70,7 +74,7 @@ def tile_contextualizer_t_kernel(tc, x, spatial_proj, out):
             out=spv[:, 4:8, :],
             in_=spatial_proj[512:1024, :].rearrange("(i p) m -> p i m", p=P),
         )
-        load_part(0, 0, 8, D, 2 * D)
+        load_first(x1_first, 0, 8, D)
         for b in range(1, B):
             load_x(b, 0, 4)
             load_x(b, 4, 4)
@@ -111,7 +115,7 @@ def tile_contextualizer_t_kernel(tc, x, spatial_proj, out):
             i0 = 2 * c
             for i in (i0, i0 + 1):
                 nc.scalar.activation(
-                    out=junk[:], in_=xs_in[b][:, i, 0:D], func=ACT.Square,
+                    out=junk[:], in_=x0_sb[b][:, i, :], func=ACT.Square,
                     accum_out=st["ss"][:, i : i + 1],
                 )
             nc.scalar.activation(
@@ -136,7 +140,7 @@ def tile_contextualizer_t_kernel(tc, x, spatial_proj, out):
             for k in range(2):
                 i = 2 * c + k
                 nc.vector.tensor_scalar(
-                    out=xn[:, k, :], in0=xs_in[b][:, i, 0:D],
+                    out=xn[:, k, :], in0=x0_sb[b][:, i, :],
                     scalar1=st["rn"][:, i : i + 1], scalar2=None, op0=ALU.mult,
                 )
 
@@ -177,7 +181,7 @@ def tile_contextualizer_t_kernel(tc, x, spatial_proj, out):
                 st["g0_%d" % g] = g0p.tile([P, D, 4], BF16, name="g0", align_bytes=64)
             g0 = st["g0_%d" % g]
             dst = g0[:, d0:d1, :].rearrange("p (c i) t -> p c t i", i=4)
-            src = xs_in[b][:, 4 * g : 4 * g + 4, d0:d1].rearrange("p t (c i) -> p c t i", i=4)
+            src = x0_sb[b][:, 4 * g : 4 * g + 4, d0:d1].rearrange("p t (c i) -> p c t i", i=4)
             if eng == "v":
                 nc.vector.tensor_copy(out=dst, in_=src)
             else:
@@ -312,7 +316,7 @@ def tile_contextualizer_t_kernel(tc, x, spatial_proj, out):
                 st["o"] = outp.tile([P, 2, D], F32, name="o")
             o = st["o"]
             nc.vector.tensor_tensor(
-                out=o[:, i % 2, :], in0=tl[s]["ctx"][:], in1=xs_in[b][:, i, D : 2 * D], op=ALU.mult,
+                out=o[:, i % 2, :], in0=tl[s]["ctx"][:], in1=x1_sb[b][:, i, :], op=ALU.mult,
             )
             if s >= NS - 2:
                 nc.sync.dma_start(out=out[b][i * P : (i + 1) * P, :], in_=o[:, i % 2, :])
@@ -351,64 +355,52 @@ def tile_contextualizer_t_kernel(tc, x, spatial_proj, out):
             mask_t(i)
 
         s_evac(1)
-        s_sumsq(3)
         v_quant_xn(1)
         mask_b(1)
-        mask_t(4, True)
-        mask_t(5, True)
+        mask_e(0)
+        pe_cosim(0)
+        mask_e(1)
+        pe_cosim(1)
         v_quant_x0(0, 1)
-        v_recip(3)
-        v_scale(3)
-        pe_transpose(3)
-        for i in range(4):
-            mask_e(i)
-        for s in range(4):
-            pe_cosim(s)
-
-        s_evac(2)
-        mask_e(4)
-        mask_e(5)
-        v_quant_xn(2)
+        mask_e(2)
+        mask_t(4)
         v_mask(0)
-        v_mask(1)
-        mask_t(6)
-        mask_t(7)
-        v_quant_attn(0)
-        v_quant_attn(1)
-        pe_ctx(0)
-        pe_ctx(1)
-        s_evac(3)
+        mask_e(3)
+        mask_t(5)
 
-        for k in range(NQ):
-            q = k + 4
+        for k in range(0, NQ + 1):
+            q = k + 3
             s_sumsq(q)
-            if k > 0:
-                s_evac(q - 1)
+            s_evac(q - 1)
             s_regroup(q)
+            if k == 0:
+                mask_e(4)
+                mask_e(5)
+
+            s = 2 * k
+            v_mask(s + 1)
+            v_quant_attn(s)
+            if k == 0:
+                pe_cosim(s + 2)
+            pe_ctx(s)
+            v_gate(s - 1)
+            if k == 0:
+                mask_t(6)
+                mask_t(7)
+
+            s = 2 * k + 1
+            v_mask(s + 1)
+            v_quant_attn(s)
+            pe_cosim(s + 2)
+            pe_ctx(s)
+            v_recip(q)
+            v_gate(s - 1)
+            if (q - 1) % 2 == 1 and q - 1 >= 4:
+                v_quant_x0((q - 1) // 4, ((q - 1) % 4) // 2)
+            v_quant_xn(q - 1)
             if k == 0:
                 mask_e(6)
                 mask_e(7)
-            v_mask(2 * k + 2)
-            v_mask(2 * k + 3)
-            pe_cosim(2 * k + 4)
-            pe_cosim(2 * k + 5)
-            if k != NQ - 2:
-                v_gate(2 * k)
-                v_gate(2 * k + 1)
-                v_recip(q)
-                v_quant_attn(2 * k + 2)
-                v_quant_attn(2 * k + 3)
-                pe_ctx(2 * k + 2)
-                pe_ctx(2 * k + 3)
-            else:
-                v_gate(2 * k)
-                v_quant_attn(2 * k + 2)
-                pe_ctx(2 * k + 2)
-                v_gate(2 * k + 1)
-                v_quant_attn(2 * k + 3)
-                pe_ctx(2 * k + 3)
-            if (q - 1) % 2 == 1 and q - 1 >= 4:
-                v_quant_x0((q - 1) // 4, ((q - 1) % 4) // 2)
+            pe_cosim(s + 3)
             v_scale(q)
             pe_transpose(q)
-            v_quant_xn(q - 1)

@@ -23,21 +23,27 @@ NQ = 4 * B
 NS = NT * B
 
 
+def ASIDE(p):
+    return 0 <= p < NQ - 1
+
+
 def tile_contextualizer_t_kernel(tc, x, spatial_proj, out):
     nc = tc.nc
     with ExitStack() as stack:
         const = stack.enter_context(tc.tile_pool(name="const", bufs=1))
         small = stack.enter_context(tc.tile_pool(name="small", bufs=2))
-        xnp = stack.enter_context(tc.tile_pool(name="xnp", bufs=3))
+        xnp = stack.enter_context(tc.tile_pool(name="xnp", bufs=4))
         gxp = stack.enter_context(tc.tile_pool(name="gxp", bufs=3))
         xqp = stack.enter_context(tc.tile_pool(name="xqp", bufs=2))
         g0p = stack.enter_context(tc.tile_pool(name="g0p", bufs=2))
         x0qp = stack.enter_context(tc.tile_pool(name="x0qp", bufs=2))
         aqp = stack.enter_context(tc.tile_pool(name="aqp", bufs=4))
         outp = stack.enter_context(tc.tile_pool(name="outp", bufs=4))
-        tp = stack.enter_context(tc.psum_pool(name="tp", bufs=2))
+        tp = stack.enter_context(tc.psum_pool(name="tp", bufs=1))
+        gpp = stack.enter_context(tc.psum_pool(name="gpp", bufs=1))
         ps1 = stack.enter_context(tc.psum_pool(name="ps1", bufs=4))
-        ps2 = stack.enter_context(tc.psum_pool(name="ps2", bufs=2))
+        ps2 = stack.enter_context(tc.psum_pool(name="ps2", bufs=1))
+        csp = stack.enter_context(tc.tile_pool(name="csp", bufs=2))
         if PIN:
             stack.enter_context(tc.manual_schedule())
 
@@ -65,11 +71,11 @@ def tile_contextualizer_t_kernel(tc, x, spatial_proj, out):
 
         load_first(x0_first, 0, 2, 0)
         load_first(x0_first, 2, 2, 0)
-        load_first(x0_first, 4, 4, 0)
         nc.sync.dma_start(
             out=spv[:, 0:4, 0:512],
             in_=spatial_proj[0:512, 0:512].rearrange("(i p) m -> p i m", p=P),
         )
+        load_first(x0_first, 4, 4, 0)
         nc.sync.dma_start(
             out=spv[:, 4:8, :],
             in_=spatial_proj[512:1024, :].rearrange("(i p) m -> p i m", p=P),
@@ -82,9 +88,11 @@ def tile_contextualizer_t_kernel(tc, x, spatial_proj, out):
         eps = const.tile([P, 1], F32, name="eps")
         nc.vector.memset(eps[:], EPS)
         warm = const.tile([P, 1], F32, name="warm")
-        nc.scalar.activation(out=warm[:], in_=eps[:], func=ACT.Sqrt)
+        nc.scalar.activation(out=warm[:], in_=eps[:], func=ACT.Abs_reciprocal_sqrt)
         ident = const.tile([P, P], BF16, name="ident")
         make_identity(nc, ident[:])
+        ident_f32 = const.tile([P, P], F32, name="ident_f32")
+        make_identity(nc, ident_f32[:])
         junk = const.tile([P, D], BF16, name="junk")
         ga_all = const.tile([P, 2, 12, 4 * P], BF16, name="ga_all", align_bytes=64)
         ga_i32 = (
@@ -110,7 +118,6 @@ def tile_contextualizer_t_kernel(tc, x, spatial_proj, out):
             st = state[b]
             if c == 0:
                 st["ss"] = small.tile([P, NT], F32, name="ss")
-                st["nrm"] = small.tile([P, NT], F32, name="nrm")
                 st["rn"] = small.tile([P, NT], F32, name="rn")
             i0 = 2 * c
             for i in (i0, i0 + 1):
@@ -119,18 +126,11 @@ def tile_contextualizer_t_kernel(tc, x, spatial_proj, out):
                     accum_out=st["ss"][:, i : i + 1],
                 )
             nc.scalar.activation(
-                out=st["nrm"][:, i0 : i0 + 2], in_=st["ss"][:, i0 : i0 + 2],
-                func=ACT.Sqrt, bias=eps[:, 0:1],
+                out=st["rn"][:, i0 : i0 + 2], in_=st["ss"][:, i0 : i0 + 2],
+                func=ACT.Abs_reciprocal_sqrt, bias=eps[:, 0:1],
             )
 
-        def v_recip(q):
-            if not 0 <= q < NQ:
-                return
-            b, c = q // 4, q % 4
-            st = state[b]
-            nc.vector.reciprocal(out=st["rn"][:, 2 * c : 2 * c + 2], in_=st["nrm"][:, 2 * c : 2 * c + 2])
-
-        def v_scale(q):
+        def scale(q):
             if not 0 <= q < NQ:
                 return
             b, c = q // 4, q % 4
@@ -148,18 +148,22 @@ def tile_contextualizer_t_kernel(tc, x, spatial_proj, out):
             if not 0 <= q < NQ:
                 return
             xn = chunk[q]["xn"]
-            xt = tp.tile([P, 8, P], BF16, name="xt")
+            xt = tp.tile([P, 4, P], F32, name="xt")
             chunk[q]["xt"] = xt
-            for k in range(2):
-                for t in range(4):
-                    nc.tensor.transpose(xt[:, 4 * k + t, :], xn[:, k, t * P : (t + 1) * P], ident[:])
+            words = xn[:].rearrange("p k d -> p (k d)").bitcast(F32)
+            for v in range(4):
+                nc.tensor.transpose(xt[:, v, :], words[:, v * P : (v + 1) * P], ident_f32[:])
 
         def s_evac(q):
             if not 0 <= q < NQ:
                 return
             gx = gxp.tile([P, 2, P, 4], BF16, name="gx", align_bytes=64)
             chunk[q]["gx"] = gx
-            nc.scalar.copy(out=gx[:], in_=chunk[q]["xt"][:].rearrange("p (k t) r -> p k r t", t=4))
+            nc.scalar.copy(
+                out=gx[:].rearrange("p k r t -> p (k r t)").bitcast(F32)
+                .rearrange("p (k r u) -> p k r u", k=2, u=2),
+                in_=chunk[q]["xt"][:].rearrange("p (k u) r -> p k r u", u=2),
+            )
 
         def v_quant_xn(q):
             if not 0 <= q < NQ:
@@ -175,23 +179,37 @@ def tile_contextualizer_t_kernel(tc, x, spatial_proj, out):
                 in_=chunk[q]["gx"][:].rearrange("p k r t -> p (k r t)"),
             )
 
-        def regroup(eng, b, g, d0, d1):
-            st = state[b]
+        def v_regroup(d0, d1):
+            st = state[0]
             if d0 == 0:
-                st["g0_%d" % g] = g0p.tile([P, D, 4], BF16, name="g0", align_bytes=64)
-            g0 = st["g0_%d" % g]
-            dst = g0[:, d0:d1, :].rearrange("p (c i) t -> p c t i", i=4)
-            src = x0_sb[b][:, 4 * g : 4 * g + 4, d0:d1].rearrange("p t (c i) -> p c t i", i=4)
-            if eng == "v":
-                nc.vector.tensor_copy(out=dst, in_=src)
-            else:
-                nc.scalar.copy(out=dst, in_=src)
+                st["g0_0"] = g0p.tile([P, D, 4], BF16, name="g0", align_bytes=64)
+            nc.vector.tensor_copy(
+                out=st["g0_0"][:, d0:d1, :].rearrange("p (c i) t -> p c t i", i=4),
+                in_=x0_first[:, 0:4, d0:d1].rearrange("p t (c i) -> p c t i", i=4),
+            )
 
-        def s_regroup(q):
-            if not 4 <= q < NQ:
+        def pe_group(q):
+            if not 2 <= q < NQ:
                 return
-            b, c = q // 4, q % 4
-            regroup("s", b, c // 2, (c % 2) * 256, (c % 2) * 256 + 256)
+            b, g, h = q // 4, q % 4 // 2, q % 2
+            gp = gpp.tile([P, 256, 4], BF16, name="gp")
+            chunk[q]["gp"] = gp
+            for d0 in (0, P):
+                c0 = 256 * h + d0
+                nc.tensor.matmul(
+                    gp[:, d0 : d0 + P, :], lhsT=ident[:],
+                    rhs=x0_sb[b][:, 4 * g : 4 * g + 4, c0 : c0 + P].rearrange("p t d -> p d t"),
+                    start=True, stop=True,
+                )
+
+        def s_group(q):
+            if not 2 <= q < NQ:
+                return
+            b, g, h = q // 4, q % 4 // 2, q % 2
+            st = state[b]
+            if h == 0:
+                st["g0_%d" % g] = g0p.tile([P, D, 4], BF16, name="g0", align_bytes=64)
+            nc.scalar.copy(out=st["g0_%d" % g][:, 256 * h : 256 * h + 256, :], in_=chunk[q]["gp"][:])
 
         def v_quant_x0(b, g):
             if not 0 <= b < B:
@@ -207,36 +225,29 @@ def tile_contextualizer_t_kernel(tc, x, spatial_proj, out):
 
         spg = {}
         pst_t = {}
-        d32 = const.tile([P, NT, P], F32, name="d32")
 
-        def mask_a(half):
-            sl = slice(4 * half, 4 * half + 4)
-            nc.vector.tensor_copy(out=d32[:, sl, :], in_=spd[:, sl, :])
-            for i in range(4 * half, 4 * half + 4):
-                nc.gpsimd.affine_select(
-                    out=d32[:, i, :], in_=d32[:, i, :], pattern=[[-1, P]],
-                    compare_op=ALU.is_ge, fill=0.0, base=0, channel_multiplier=1,
-                )
+        def mask_sel(half):
+            dia = spd[:, 4 * half : 4 * half + 4, :]
+            nc.gpsimd.affine_select(
+                out=dia, in_=dia, pattern=[[0, 4], [-1, P]],
+                compare_op=ALU.is_ge, fill=0.0, base=0, channel_multiplier=1,
+            )
 
-        def mask_b(half):
-            sl = slice(4 * half, 4 * half + 4)
-            nc.vector.tensor_copy(out=spd[:, sl, :], in_=d32[:, sl, :])
-
-        def mask_t(i, in_ctx_banks=False):
-            if in_ctx_banks:
-                pst = ps2.tile([P, 8, P], BF16, name="pst2", tag="ctxp")
-            else:
-                pst = ps1.tile([P, 8, P], BF16, name="pst", tag="c1")
-            pst_t[i] = pst
-            for j in range(i + 1):
-                nc.tensor.transpose(pst[:, j, :], spv[:, i, j * P : (j + 1) * P], ident[:])
+        def mask_t(rows, pool, tag):
+            pst = pool.tile([P, 8, P], BF16, name="pst", tag=tag)
+            n = 0
+            for i in rows:
+                pst_t[i] = pst[:, n : n + i + 1, :]
+                for j in range(i + 1):
+                    nc.tensor.transpose(pst[:, n + j, :], spv[:, i, j * P : (j + 1) * P], ident[:])
+                n += i + 1
 
         def mask_e(i):
             for g in range(i // 4 + 1):
                 T = min(i - 4 * g, 3) + 1
                 sg = const.tile([P, P, T], BF16, name="spg%d_%d" % (i, g))
                 src = pst_t[i][:, 4 * g : 4 * g + T, :].rearrange("p t n -> p n t")
-                if i >= 4:
+                if i >= 6:
                     nc.scalar.copy(out=sg[:], in_=src)
                 else:
                     nc.vector.tensor_copy(out=sg[:], in_=src)
@@ -277,18 +288,19 @@ def tile_contextualizer_t_kernel(tc, x, spatial_proj, out):
                     op=ALU.mult,
                 )
 
-        def v_quant_attn(s):
+        def v_quant_attn(s, n):
             if not 0 <= s < NS:
                 return
             b, i = s // NT, s % NT
-            ng = i // 4 + 1
-            aq = aqp.tile([P, 2, P], U32, name="aq", align_bytes=64)
-            asc = aqp.tile([P, 2, P], U8, name="asc", align_bytes=64)
-            tl[s]["aq"], tl[s]["asc"] = aq, asc
+            u0, nu = unit0(i), n * (i // 4 + 1)
+            aq = aqp.tile([P, 4, P], U32, name="aq", align_bytes=64)
+            asc = aqp.tile([P, 4, P], U8, name="asc", align_bytes=64)
+            for k in range(n):
+                tl[s + k]["aq"], tl[s + k]["asc"], tl[s + k]["u"] = aq, asc, k * (i // 4 + 1)
             nc.vector.quantize_mx(
-                out=aq[:, 0:ng, :].rearrange("p g n -> p (g n)").bitcast(FP8X4),
-                scales=asc[:, 0:ng, :].rearrange("p g n -> p (g n)"),
-                in_=ga_all[:, b % 2, unit0(i) : unit0(i) + ng, :].rearrange("p u c -> p (u c)"),
+                out=aq[:, 0:nu, :].rearrange("p u n -> p (u n)").bitcast(FP8X4),
+                scales=asc[:, 0:nu, :].rearrange("p u n -> p (u n)"),
+                in_=ga_all[:, b % 2, u0 : u0 + nu, :].rearrange("p u c -> p (u c)"),
             )
 
         def pe_ctx(s):
@@ -297,110 +309,110 @@ def tile_contextualizer_t_kernel(tc, x, spatial_proj, out):
             b, i = s // NT, s % NT
             st = state[b]
             ng = i // 4 + 1
-            ctxp = ps2.tile([P, D], F32, name="ctxp", tag="ctxp")
+            tag = "ctx%d" % (i % 2)
+            ctxp = ps2.tile([P, D], F32, name="ctxp", tag=tag)
             tl[s]["ctx"] = ctxp
             for g in range(ng):
+                u = tl[s]["u"] + g
                 nc.tensor.matmul_mx(
                     out=ctxp[:],
-                    lhsT=tl[s]["aq"][:, g, :].bitcast(FP8X4), lhsT_scale=tl[s]["asc"][:, g, :],
+                    lhsT=tl[s]["aq"][:, u, :].bitcast(FP8X4), lhsT_scale=tl[s]["asc"][:, u, :],
                     rhs=st["x0q"][:, g, :].bitcast(FP8X4), rhs_scale=st["x0s"][:, g, :],
                     start=(g == 0), stop=(g == ng - 1),
                 )
 
-        def v_gate(s):
+        def gate(s, aside):
             if not 0 <= s < NS:
                 return
             b, i = s // NT, s % NT
             st = state[b]
-            if i % 2 == 0:
-                st["o"] = outp.tile([P, 2, D], F32, name="o")
-            o = st["o"]
-            nc.vector.tensor_tensor(
-                out=o[:, i % 2, :], in0=tl[s]["ctx"][:], in1=x1_sb[b][:, i, :], op=ALU.mult,
-            )
-            if s >= NS - 2:
-                nc.sync.dma_start(out=out[b][i * P : (i + 1) * P, :], in_=o[:, i % 2, :])
-            elif i % 2 == 1:
-                nc.sync.dma_start(
-                    out=out[b][(i - 1) * P : (i + 1) * P, :].rearrange("(i p) d -> p i d", p=P),
-                    in_=o[:],
+            if "o" not in tl[s]:
+                o = outp.tile([P, 2, D], F32, name="o")
+                tl[s - s % 2]["o"], tl[s - s % 2 + 1]["o"] = o, o
+            o = tl[s]["o"]
+            if aside:
+                cs = csp.tile([P, D], F32, name="cs")
+                nc.scalar.copy(out=cs[:], in_=tl[s]["ctx"][:])
+                nc.gpsimd.tensor_tensor(out=o[:, i % 2, :], in0=cs[:], in1=x1_sb[b][:, i, :], op=ALU.mult)
+            else:
+                nc.vector.tensor_tensor(
+                    out=o[:, i % 2, :], in0=tl[s]["ctx"][:], in1=x1_sb[b][:, i, :], op=ALU.mult,
                 )
+
+        def store(s, n):
+            if not 0 <= s < NS:
+                return
+            b, i = s // NT, s % NT
+            nc.sync.dma_start(
+                out=out[b][i * P : (i + n) * P, :].rearrange("(i p) d -> p i d", p=P),
+                in_=tl[s]["o"][:, i % 2 : i % 2 + n, :],
+            )
 
         H2 = D // 2
         s_sumsq(0)
-        regroup("v", 0, 0, 0, H2)
-        v_recip(0)
-        v_scale(0)
+        scale(0)
         pe_transpose(0)
-
         s_sumsq(1)
-        regroup("v", 0, 0, H2, D)
-        v_recip(1)
-        v_scale(1)
+        v_regroup(0, H2)
+        scale(1)
         pe_transpose(1)
-        mask_a(0)
-        v_quant_x0(0, 0)
-
+        mask_sel(0)
+        mask_sel(1)
         s_evac(0)
+        v_regroup(H2, D)
+        mask_t((0, 1, 2), ps1, "c1")
+        mask_t((3,), ps1, "c1")
         s_sumsq(2)
-        mask_a(1)
+        for i in range(3):
+            mask_e(i)
         v_quant_xn(0)
-        regroup("v", 0, 1, 0, H2)
-        v_recip(2)
-        v_scale(2)
-        pe_transpose(2)
-        regroup("v", 0, 1, H2, D)
-        mask_b(0)
-        for i in range(4):
-            mask_t(i)
-
-        s_evac(1)
-        v_quant_xn(1)
-        mask_b(1)
-        mask_e(0)
-        pe_cosim(0)
-        mask_e(1)
-        pe_cosim(1)
-        v_quant_x0(0, 1)
-        mask_e(2)
-        mask_t(4)
-        v_mask(0)
         mask_e(3)
-        mask_t(5)
+        pe_cosim(0)
+        pe_cosim(1)
+        s_evac(1)
+        scale(2)
+        v_quant_x0(0, 0)
+        pe_transpose(2)
+        mask_t((4,), ps1, "c1")
+        mask_t((5,), ps1, "c1")
+        mask_t((6,), gpp, "gp")
+        mask_t((7,), ps2, "ctx1")
+        s_sumsq(3)
+        s_evac(2)
+        mask_e(6)
+        s_sumsq(4)
+        mask_e(7)
 
-        for k in range(0, NQ + 1):
-            q = k + 3
-            s_sumsq(q)
-            s_evac(q - 1)
-            s_regroup(q)
-            if k == 0:
+        for p in range(-1, NQ + 1):
+            v_mask(2 * p + 2)
+            v_mask(2 * p + 3)
+            v_quant_xn(p + 2)
+            pe_cosim(2 * p + 4)
+            pe_cosim(2 * p + 5)
+            if p == -1:
                 mask_e(4)
+            if p != 0:
+                scale(p + 4)
+            if p == -1:
                 mask_e(5)
-
-            s = 2 * k
-            v_mask(s + 1)
-            v_quant_attn(s)
-            if k == 0:
-                pe_cosim(s + 2)
-            pe_ctx(s)
-            v_gate(s - 1)
-            if k == 0:
-                mask_t(6)
-                mask_t(7)
-
-            s = 2 * k + 1
-            v_mask(s + 1)
-            v_quant_attn(s)
-            pe_cosim(s + 2)
-            pe_ctx(s)
-            v_recip(q)
-            v_gate(s - 1)
-            if (q - 1) % 2 == 1 and q - 1 >= 4:
-                v_quant_x0((q - 1) // 4, ((q - 1) % 4) // 2)
-            v_quant_xn(q - 1)
-            if k == 0:
-                mask_e(6)
-                mask_e(7)
-            pe_cosim(s + 3)
-            v_scale(q)
-            pe_transpose(q)
+            if p >= 0:
+                s_evac(p + 3)
+                s_sumsq(p + 5)
+                pe_group(p + 2)
+                s_group(p + 2)
+            if p != 0:
+                pe_transpose(p + 4)
+            if p % 2 == 0 and p > 0:
+                v_quant_x0((p + 1) // 4, ((p + 1) % 4) // 2)
+            v_quant_attn(2 * p, 2)
+            if not ASIDE(p - 1):
+                gate(2 * p - 1, False)
+            gate(2 * p - 2, False)
+            pe_ctx(2 * p + 1)
+            if ASIDE(p):
+                gate(2 * p + 1, True)
+            pe_ctx(2 * p)
+            store(2 * p - 2, 2)
+            if p == 0:
+                scale(p + 4)
+                pe_transpose(p + 4)

@@ -24,7 +24,7 @@ NS = NT * B
 
 
 def ASIDE(p):
-    return 0 <= p < NQ - 1
+    return 0 <= p < NQ - 1 and p % 4 < 2
 
 
 def tile_contextualizer_t_kernel(tc, x, spatial_proj, out):

@@ -24,13 +24,22 @@ NS = NT * B
 
 
 def ASIDE(p):
-    return 0 <= p < NQ - 1 and p % 4 < 2
+    return False
+
+
+def SSC(q):
+    return q >= 5 and q % 4 >= 2
+
+
+def PLACE(p):
+    return False
 
 
 def tile_contextualizer_t_kernel(tc, x, spatial_proj, out):
     nc = tc.nc
     with ExitStack() as stack:
         const = stack.enter_context(tc.tile_pool(name="const", bufs=1))
+        junkp = stack.enter_context(tc.tile_pool(name="junkp", bufs=4))
         small = stack.enter_context(tc.tile_pool(name="small", bufs=2))
         xnp = stack.enter_context(tc.tile_pool(name="xnp", bufs=4))
         gxp = stack.enter_context(tc.tile_pool(name="gxp", bufs=3))
@@ -43,6 +52,7 @@ def tile_contextualizer_t_kernel(tc, x, spatial_proj, out):
         gpp = stack.enter_context(tc.psum_pool(name="gpp", bufs=1))
         ps1 = stack.enter_context(tc.psum_pool(name="ps1", bufs=4))
         ps2 = stack.enter_context(tc.psum_pool(name="ps2", bufs=1))
+        dgp = stack.enter_context(tc.tile_pool(name="dgp", bufs=2))
         csp = stack.enter_context(tc.tile_pool(name="csp", bufs=2))
         if PIN:
             stack.enter_context(tc.manual_schedule())
@@ -69,7 +79,8 @@ def tile_contextualizer_t_kernel(tc, x, spatial_proj, out):
                 in_=x[0][i0 * P : (i0 + n) * P, c0 : c0 + D].rearrange("(i p) c -> p i c", p=P),
             )
 
-        load_first(x0_first, 0, 2, 0)
+        load_first(x0_first, 0, 1, 0)
+        load_first(x0_first, 1, 1, 0)
         load_first(x0_first, 2, 2, 0)
         nc.sync.dma_start(
             out=spv[:, 0:4, 0:512],
@@ -93,7 +104,6 @@ def tile_contextualizer_t_kernel(tc, x, spatial_proj, out):
         make_identity(nc, ident[:])
         ident_f32 = const.tile([P, P], F32, name="ident_f32")
         make_identity(nc, ident_f32[:])
-        junk = const.tile([P, D], BF16, name="junk")
         ga_all = const.tile([P, 2, 12, 4 * P], BF16, name="ga_all", align_bytes=64)
         ga_i32 = (
             ga_all[:].rearrange("p a u c -> p (a u c)").bitcast(I32)
@@ -121,6 +131,13 @@ def tile_contextualizer_t_kernel(tc, x, spatial_proj, out):
                 st["rn"] = small.tile([P, NT], F32, name="rn")
             i0 = 2 * c
             for i in (i0, i0 + 1):
+                junk = junkp.tile([P, D], BF16, name="junk")
+                if q == 0 and i == 1:
+                    nc.vector.scalar_tensor_tensor(
+                        out=junk[:], in0=x0_sb[b][:, i, :], scalar=1.0, in1=x0_sb[b][:, i, :],
+                        op0=ALU.mult, op1=ALU.mult, accum_out=st["ss"][:, i : i + 1],
+                    )
+                    continue
                 nc.scalar.activation(
                     out=junk[:], in_=x0_sb[b][:, i, :], func=ACT.Square,
                     accum_out=st["ss"][:, i : i + 1],
@@ -130,14 +147,29 @@ def tile_contextualizer_t_kernel(tc, x, spatial_proj, out):
                 func=ACT.Abs_reciprocal_sqrt, bias=eps[:, 0:1],
             )
 
-        def scale(q):
+        def s_scale(q, ks):
             if not 0 <= q < NQ:
                 return
             b, c = q // 4, q % 4
             st = state[b]
             xn = xnp.tile([P, 2, D], BF16, name="xn")
             chunk[q]["xn"] = xn
-            for k in range(2):
+            for k in ks:
+                i = 2 * c + k
+                nc.scalar.activation(
+                    out=xn[:, k, :], in_=x0_sb[b][:, i, :],
+                    func=ACT.Copy, scale=st["rn"][:, i : i + 1],
+                )
+
+        def scale(q, ks=(0, 1)):
+            if not 0 <= q < NQ:
+                return
+            b, c = q // 4, q % 4
+            st = state[b]
+            if "xn" not in chunk[q]:
+                chunk[q]["xn"] = xnp.tile([P, 2, D], BF16, name="xn")
+            xn = chunk[q]["xn"]
+            for k in ks:
                 i = 2 * c + k
                 nc.vector.tensor_scalar(
                     out=xn[:, k, :], in0=x0_sb[b][:, i, :],
@@ -280,13 +312,22 @@ def tile_contextualizer_t_kernel(tc, x, spatial_proj, out):
             b, i = s // NT, s % NT
             for g in range(i // 4 + 1):
                 T = min(i - 4 * g, 3) + 1
-                ga = ga_all[:, b % 2, unit0(i) + g, :].rearrange("p (n t) -> p n t", t=4)
+                ga = ga_all[:, b % 2, unit0(i) + g, :].rearrange("p (n t) -> p n t", t=4)[:, :, 0:T]
+                if T <= 2 and s > 1:
+                    tl[s]["place"] = ga
+                    ga = dgp.tile([P, P, T], BF16, name="dg%d" % T)
+                    tl[s]["dg"] = ga
                 nc.vector.tensor_tensor(
-                    out=ga[:, :, 0:T],
+                    out=ga[:],
                     in0=tl[s]["c1"][g][:, 0:T, :].rearrange("p t n -> p n t"),
                     in1=spg[(i, g)][:],
                     op=ALU.mult,
                 )
+
+        def s_place(s):
+            if not 0 <= s < NS or "place" not in tl[s]:
+                return
+            nc.scalar.copy(out=tl[s]["place"], in_=tl[s]["dg"][:])
 
         def v_quant_attn(s, n):
             if not 0 <= s < NS:
@@ -382,6 +423,7 @@ def tile_contextualizer_t_kernel(tc, x, spatial_proj, out):
         mask_e(6)
         s_sumsq(4)
         mask_e(7)
+        s_sumsq(5)
 
         for p in range(-1, NQ + 1):
             v_mask(2 * p + 2)
@@ -392,27 +434,42 @@ def tile_contextualizer_t_kernel(tc, x, spatial_proj, out):
             if p == -1:
                 mask_e(4)
             if p != 0:
-                scale(p + 4)
+                scale(p + 4, (1,) if SSC(p + 4) else (0, 1))
             if p == -1:
                 mask_e(5)
             if p >= 0:
                 s_evac(p + 3)
-                s_sumsq(p + 5)
+            s_place(2 * p + 2)
+            s_place(2 * p + 3)
+            if p >= 0:
                 pe_group(p + 2)
                 s_group(p + 2)
+                if SSC(p + 5):
+                    s_scale(p + 5, (0,))
+                s_sumsq(p + 6)
             if p != 0:
                 pe_transpose(p + 4)
             if p % 2 == 0 and p > 0:
                 v_quant_x0((p + 1) // 4, ((p + 1) % 4) // 2)
-            v_quant_attn(2 * p, 2)
+            if p == NQ - 1:
+                v_quant_attn(2 * p, 1)
+            else:
+                v_quant_attn(2 * p, 2)
+            if p == NQ - 1:
+                v_quant_attn(2 * p + 1, 1)
+            gate(2 * p - 2, False)
+            pe_ctx(2 * p)
+            if p == NQ:
+                store(2 * p - 2, 1)
             if not ASIDE(p - 1):
                 gate(2 * p - 1, False)
-            gate(2 * p - 2, False)
             pe_ctx(2 * p + 1)
             if ASIDE(p):
                 gate(2 * p + 1, True)
-            pe_ctx(2 * p)
-            store(2 * p - 2, 2)
+            if p == NQ:
+                store(2 * p - 1, 1)
+            else:
+                store(2 * p - 2, 2)
             if p == 0:
                 scale(p + 4)
                 pe_transpose(p + 4)

@@ -24,11 +24,11 @@ NS = NT * B
 
 
 def ASIDE(p):
-    return False
+    return 4 <= p < NQ - 1 and p % 4 in (0, 3)
 
 
 def SSC(q):
-    return q >= 5 and q % 4 >= 2
+    return (0,) if q >= 5 and q % 4 >= 2 else ()
 
 
 def PLACE(p):
@@ -79,8 +79,7 @@ def tile_contextualizer_t_kernel(tc, x, spatial_proj, out):
                 in_=x[0][i0 * P : (i0 + n) * P, c0 : c0 + D].rearrange("(i p) c -> p i c", p=P),
             )
 
-        load_first(x0_first, 0, 1, 0)
-        load_first(x0_first, 1, 1, 0)
+        load_first(x0_first, 0, 2, 0)
         load_first(x0_first, 2, 2, 0)
         nc.sync.dma_start(
             out=spv[:, 0:4, 0:512],
@@ -121,7 +120,7 @@ def tile_contextualizer_t_kernel(tc, x, spatial_proj, out):
         chunk = [dict() for q in range(NQ)]
         tl = [dict() for s in range(NS)]
 
-        def s_sumsq(q):
+        def s_sumsq(q, fin=True):
             if not 0 <= q < NQ:
                 return
             b, c = q // 4, q % 4
@@ -142,6 +141,13 @@ def tile_contextualizer_t_kernel(tc, x, spatial_proj, out):
                     out=junk[:], in_=x0_sb[b][:, i, :], func=ACT.Square,
                     accum_out=st["ss"][:, i : i + 1],
                 )
+            if fin:
+                s_rsq(q)
+
+        def s_rsq(q):
+            if not 0 <= q < NQ:
+                return
+            st, i0 = state[q // 4], 2 * (q % 4)
             nc.scalar.activation(
                 out=st["rn"][:, i0 : i0 + 2], in_=st["ss"][:, i0 : i0 + 2],
                 func=ACT.Abs_reciprocal_sqrt, bias=eps[:, 0:1],
@@ -152,8 +158,9 @@ def tile_contextualizer_t_kernel(tc, x, spatial_proj, out):
                 return
             b, c = q // 4, q % 4
             st = state[b]
-            xn = xnp.tile([P, 2, D], BF16, name="xn")
-            chunk[q]["xn"] = xn
+            if "xn" not in chunk[q]:
+                chunk[q]["xn"] = xnp.tile([P, 2, D], BF16, name="xn")
+            xn = chunk[q]["xn"]
             for k in ks:
                 i = 2 * c + k
                 nc.scalar.activation(
@@ -362,6 +369,11 @@ def tile_contextualizer_t_kernel(tc, x, spatial_proj, out):
                     start=(g == 0), stop=(g == ng - 1),
                 )
 
+        def s_take(s):
+            cs = csp.tile([P, D], F32, name="cs")
+            tl[s]["cs"] = cs
+            nc.scalar.copy(out=cs[:], in_=tl[s]["ctx"][:])
+
         def gate(s, aside):
             if not 0 <= s < NS:
                 return
@@ -372,9 +384,10 @@ def tile_contextualizer_t_kernel(tc, x, spatial_proj, out):
                 tl[s - s % 2]["o"], tl[s - s % 2 + 1]["o"] = o, o
             o = tl[s]["o"]
             if aside:
-                cs = csp.tile([P, D], F32, name="cs")
-                nc.scalar.copy(out=cs[:], in_=tl[s]["ctx"][:])
-                nc.gpsimd.tensor_tensor(out=o[:, i % 2, :], in0=cs[:], in1=x1_sb[b][:, i, :], op=ALU.mult)
+                tl[s]["row"] = xs_in[b][:, i - 1, :].bitcast(F32)
+                nc.gpsimd.tensor_tensor(
+                    out=tl[s]["row"], in0=tl[s]["cs"][:], in1=x1_sb[b][:, i, :], op=ALU.mult,
+                )
             else:
                 nc.vector.tensor_tensor(
                     out=o[:, i % 2, :], in0=tl[s]["ctx"][:], in1=x1_sb[b][:, i, :], op=ALU.mult,
@@ -384,10 +397,13 @@ def tile_contextualizer_t_kernel(tc, x, spatial_proj, out):
             if not 0 <= s < NS:
                 return
             b, i = s // NT, s % NT
-            nc.sync.dma_start(
-                out=out[b][i * P : (i + n) * P, :].rearrange("(i p) d -> p i d", p=P),
-                in_=tl[s]["o"][:, i % 2 : i % 2 + n, :],
-            )
+            if "row" in tl[s]:
+                nc.sync.dma_start(out=out[b][i * P : (i + 1) * P, :], in_=tl[s]["row"])
+            else:
+                nc.sync.dma_start(
+                    out=out[b][i * P : (i + n) * P, :].rearrange("(i p) d -> p i d", p=P),
+                    in_=tl[s]["o"][:, i % 2 : i % 2 + n, :],
+                )
 
         H2 = D // 2
         s_sumsq(0)
@@ -434,23 +450,22 @@ def tile_contextualizer_t_kernel(tc, x, spatial_proj, out):
             if p == -1:
                 mask_e(4)
             if p != 0:
-                scale(p + 4, (1,) if SSC(p + 4) else (0, 1))
+                scale(p + 4, [k for k in range(2) if k not in SSC(p + 4)])
             if p == -1:
                 mask_e(5)
             if p >= 0:
                 s_evac(p + 3)
+                if p > 0:
+                    s_rsq(p + 5)
             s_place(2 * p + 2)
             s_place(2 * p + 3)
             if p >= 0:
                 pe_group(p + 2)
                 s_group(p + 2)
-                if SSC(p + 5):
-                    s_scale(p + 5, (0,))
-                s_sumsq(p + 6)
+                s_scale(p + 5, SSC(p + 5))
+                s_sumsq(p + 6, False)
             if p != 0:
                 pe_transpose(p + 4)
-            if p % 2 == 0 and p > 0:
-                v_quant_x0((p + 1) // 4, ((p + 1) % 4) // 2)
             if p == NQ - 1:
                 v_quant_attn(2 * p, 1)
             else:
@@ -458,15 +473,22 @@ def tile_contextualizer_t_kernel(tc, x, spatial_proj, out):
             if p == NQ - 1:
                 v_quant_attn(2 * p + 1, 1)
             gate(2 * p - 2, False)
-            pe_ctx(2 * p)
             if p == NQ:
                 store(2 * p - 2, 1)
-            if not ASIDE(p - 1):
-                gate(2 * p - 1, False)
+            if p % 2 == 0 and p > 0:
+                gate(2 * p - 1, ASIDE(p - 1))
+                v_quant_x0((p + 1) // 4, ((p + 1) % 4) // 2)
+                pe_ctx(2 * p)
+            else:
+                pe_ctx(2 * p)
+                gate(2 * p - 1, ASIDE(p - 1))
             pe_ctx(2 * p + 1)
             if ASIDE(p):
-                gate(2 * p + 1, True)
+                s_take(2 * p + 1)
             if p == NQ:
+                store(2 * p - 1, 1)
+            elif ASIDE(p - 1):
+                store(2 * p - 2, 1)
                 store(2 * p - 1, 1)
             else:
                 store(2 * p - 2, 2)

@@ -28,7 +28,7 @@ def ASIDE(p):
 
 
 def SSC(q):
-    return (0,) if q >= 5 and q % 4 >= 2 else ()
+    return (0,) if q >= 5 else ()
 
 
 def PLACE(p):
@@ -100,18 +100,17 @@ def tile_contextualizer_t_kernel(tc, x, spatial_proj, out):
         warm = const.tile([P, 1], F32, name="warm")
         nc.scalar.activation(out=warm[:], in_=eps[:], func=ACT.Abs_reciprocal_sqrt)
         ident = const.tile([P, P], BF16, name="ident")
-        make_identity(nc, ident[:])
         ident_f32 = const.tile([P, P], F32, name="ident_f32")
         make_identity(nc, ident_f32[:])
+        make_identity(nc, ident[:])
         ga_all = const.tile([P, 2, 12, 4 * P], BF16, name="ga_all", align_bytes=64)
         ga_i32 = (
             ga_all[:].rearrange("p a u c -> p (a u c)").bitcast(I32)
             .rearrange("p (a u w) -> p a u w", a=2, u=12)
         )
         nc.vector.memset(ga_i32[:, :, 0:3, :], 0)
-        nc.vector.memset(
-            ga_i32[:, :, 4:12, :].rearrange("p a (i g) w -> p a i g w", g=2)[:, :, 0:3, 1, :], 0
-        )
+        ga_diag = ga_i32[:, :, 4:12, :].rearrange("p a (i g) w -> p a i g w", g=2)[:, :, 0:3, 1, :]
+        nc.vector.memset(ga_diag[:, 0], 0)
 
         def unit0(i):
             return i if i < 4 else 4 + 2 * (i - 4)
@@ -407,25 +406,26 @@ def tile_contextualizer_t_kernel(tc, x, spatial_proj, out):
 
         H2 = D // 2
         s_sumsq(0)
+        nc.vector.memset(ga_diag[:, 1], 0)
         scale(0)
         pe_transpose(0)
         s_sumsq(1)
+        s_evac(0)
         v_regroup(0, H2)
+        mask_sel(0)
+        mask_t((0, 1, 2), ps1, "c1")
         scale(1)
         pe_transpose(1)
-        mask_sel(0)
         mask_sel(1)
-        s_evac(0)
-        v_regroup(H2, D)
-        mask_t((0, 1, 2), ps1, "c1")
         mask_t((3,), ps1, "c1")
-        s_sumsq(2)
+        v_regroup(H2, D)
         for i in range(3):
             mask_e(i)
+        s_sumsq(2)
         v_quant_xn(0)
-        mask_e(3)
         pe_cosim(0)
         pe_cosim(1)
+        mask_e(3)
         s_evac(1)
         scale(2)
         v_quant_x0(0, 0)

@@ -28,7 +28,7 @@ def ASIDE(p):
 
 
 def SSC(q):
-    return (0,) if q >= 5 else ()
+    return (0,) if q >= 5 and q % 4 >= 2 else ()
 
 
 def PLACE(p):
@@ -357,7 +357,10 @@ def tile_contextualizer_t_kernel(tc, x, spatial_proj, out):
             st = state[b]
             ng = i // 4 + 1
             tag = "ctx%d" % (i % 2)
-            ctxp = ps2.tile([P, D], F32, name="ctxp", tag=tag)
+            if s < NS - 2:
+                ctxp = ps2.tile([P, D], F32, name="ctxp", tag=tag)
+            else:
+                ctxp = ps1.tile([P, D], F32, name="ctxl", tag="c1")
             tl[s]["ctx"] = ctxp
             for g in range(ng):
                 u = tl[s]["u"] + g
@@ -391,6 +394,13 @@ def tile_contextualizer_t_kernel(tc, x, spatial_proj, out):
                 nc.vector.tensor_tensor(
                     out=o[:, i % 2, :], in0=tl[s]["ctx"][:], in1=x1_sb[b][:, i, :], op=ALU.mult,
                 )
+
+        def gate_part(s, c):
+            b, i = s // NT, s % NT
+            cols = slice(c, c + D // 2)
+            o = tl[s]["o"][:, 1, cols]
+            nc.vector.tensor_tensor(out=o, in0=tl[s]["ctx"][:, cols], in1=x1_sb[b][:, i, cols], op=ALU.mult)
+            nc.sync.dma_start(out=out[b][i * P : (i + 1) * P, cols], in_=o)
 
         def store(s, n):
             if not 0 <= s < NS:
@@ -472,12 +482,19 @@ def tile_contextualizer_t_kernel(tc, x, spatial_proj, out):
                 v_quant_attn(2 * p, 2)
             if p == NQ - 1:
                 v_quant_attn(2 * p + 1, 1)
+            if p % 2 == 0 and p > 0 and p == NQ - 2:
+                v_quant_x0((p + 1) // 4, ((p + 1) % 4) // 2)
             gate(2 * p - 2, False)
-            if p == NQ:
+            if p >= NQ - 1:
                 store(2 * p - 2, 1)
+            if p == NQ:
+                for c in (0, D // 2):
+                    gate_part(NS - 1, c)
+                break
             if p % 2 == 0 and p > 0:
                 gate(2 * p - 1, ASIDE(p - 1))
-                v_quant_x0((p + 1) // 4, ((p + 1) % 4) // 2)
+                if not (p == NQ - 2):
+                    v_quant_x0((p + 1) // 4, ((p + 1) % 4) // 2)
                 pe_ctx(2 * p)
             else:
                 pe_ctx(2 * p)
@@ -485,7 +502,7 @@ def tile_contextualizer_t_kernel(tc, x, spatial_proj, out):
             pe_ctx(2 * p + 1)
             if ASIDE(p):
                 s_take(2 * p + 1)
-            if p == NQ:
+            if p == NQ - 1:
                 store(2 * p - 1, 1)
             elif ASIDE(p - 1):
                 store(2 * p - 2, 1)

@@ -28,7 +28,7 @@ def ASIDE(p):
 
 
 def SSC(q):
-    return (0,) if q >= 5 and q % 4 >= 2 else ()
+    return ()
 
 
 def PLACE(p):
@@ -49,8 +49,7 @@ def tile_contextualizer_t_kernel(tc, x, spatial_proj, out):
         aqp = stack.enter_context(tc.tile_pool(name="aqp", bufs=4))
         outp = stack.enter_context(tc.tile_pool(name="outp", bufs=4))
         tp = stack.enter_context(tc.psum_pool(name="tp", bufs=1))
-        gpp = stack.enter_context(tc.psum_pool(name="gpp", bufs=1))
-        ps1 = stack.enter_context(tc.psum_pool(name="ps1", bufs=4))
+        ps1 = stack.enter_context(tc.psum_pool(name="ps1", bufs=5))
         ps2 = stack.enter_context(tc.psum_pool(name="ps2", bufs=1))
         dgp = stack.enter_context(tc.tile_pool(name="dgp", bufs=2))
         csp = stack.enter_context(tc.tile_pool(name="csp", bufs=2))
@@ -226,20 +225,6 @@ def tile_contextualizer_t_kernel(tc, x, spatial_proj, out):
                 in_=x0_first[:, 0:4, d0:d1].rearrange("p t (c i) -> p c t i", i=4),
             )
 
-        def pe_group(q):
-            if not 2 <= q < NQ:
-                return
-            b, g, h = q // 4, q % 4 // 2, q % 2
-            gp = gpp.tile([P, 256, 4], BF16, name="gp")
-            chunk[q]["gp"] = gp
-            for d0 in (0, P):
-                c0 = 256 * h + d0
-                nc.tensor.matmul(
-                    gp[:, d0 : d0 + P, :], lhsT=ident[:],
-                    rhs=x0_sb[b][:, 4 * g : 4 * g + 4, c0 : c0 + P].rearrange("p t d -> p d t"),
-                    start=True, stop=True,
-                )
-
         def s_group(q):
             if not 2 <= q < NQ:
                 return
@@ -247,7 +232,13 @@ def tile_contextualizer_t_kernel(tc, x, spatial_proj, out):
             st = state[b]
             if h == 0:
                 st["g0_%d" % g] = g0p.tile([P, D, 4], BF16, name="g0", align_bytes=64)
-            nc.scalar.copy(out=st["g0_%d" % g][:, 256 * h : 256 * h + 256, :], in_=chunk[q]["gp"][:])
+            cols = slice(256 * h, 256 * h + 256)
+            dst = st["g0_%d" % g][:, cols, :].rearrange("p (c i) t -> p c t i", i=4)
+            src = x0_sb[b][:, 4 * g : 4 * g + 4, cols].rearrange("p t (c i) -> p c t i", i=4)
+            if False:
+                nc.vector.tensor_copy(out=dst, in_=src)
+            else:
+                nc.scalar.copy(out=dst, in_=src)
 
         def v_quant_x0(b, g):
             if not 0 <= b < B:
@@ -442,7 +433,7 @@ def tile_contextualizer_t_kernel(tc, x, spatial_proj, out):
         pe_transpose(2)
         mask_t((4,), ps1, "c1")
         mask_t((5,), ps1, "c1")
-        mask_t((6,), gpp, "gp")
+        mask_t((6,), ps1, "c1")
         mask_t((7,), ps2, "ctx1")
         s_sumsq(3)
         s_evac(2)
@@ -470,7 +461,6 @@ def tile_contextualizer_t_kernel(tc, x, spatial_proj, out):
             s_place(2 * p + 2)
             s_place(2 * p + 3)
             if p >= 0:
-                pe_group(p + 2)
                 s_group(p + 2)
                 s_scale(p + 5, SSC(p + 5))
                 s_sumsq(p + 6, False)

@@ -24,11 +24,15 @@ NS = NT * B
 
 
 def ASIDE(p):
-    return 4 <= p < NQ - 1 and p % 4 in (0, 3)
+    return 0 < p < NQ - 1 and p % 4 in (0, 3)
+
+
+def EARLY(p):
+    return p in (4, 8, 12)
 
 
 def SSC(q):
-    return ()
+    return (0,) if q >= 5 and q % 4 == 3 else ()
 
 
 def PLACE(p):
@@ -326,6 +330,11 @@ def tile_contextualizer_t_kernel(tc, x, spatial_proj, out):
                 return
             nc.scalar.copy(out=tl[s]["place"], in_=tl[s]["dg"][:])
 
+        def g_place(s):
+            nc.gpsimd.tensor_scalar(
+                out=tl[s]["place"], in0=tl[s]["dg"][:], scalar1=1.0, scalar2=0.0, op0=ALU.mult, op1=ALU.add,
+            )
+
         def v_quant_attn(s, n):
             if not 0 <= s < NS:
                 return
@@ -348,7 +357,7 @@ def tile_contextualizer_t_kernel(tc, x, spatial_proj, out):
             st = state[b]
             ng = i // 4 + 1
             tag = "ctx%d" % (i % 2)
-            if s < NS - 2:
+            if s < NS - 4:
                 ctxp = ps2.tile([P, D], F32, name="ctxp", tag=tag)
             else:
                 ctxp = ps1.tile([P, D], F32, name="ctxl", tag="c1")
@@ -377,7 +386,10 @@ def tile_contextualizer_t_kernel(tc, x, spatial_proj, out):
                 tl[s - s % 2]["o"], tl[s - s % 2 + 1]["o"] = o, o
             o = tl[s]["o"]
             if aside:
-                tl[s]["row"] = xs_in[b][:, i - 1, :].bitcast(F32)
+                if b == 0:
+                    tl[s]["row"] = x1_first[:, i - 2 : i, :].rearrange("p i d -> p (i d)").bitcast(F32)
+                else:
+                    tl[s]["row"] = xs_in[b][:, i - 1, :].bitcast(F32)
                 nc.gpsimd.tensor_tensor(
                     out=tl[s]["row"], in0=tl[s]["cs"][:], in1=x1_sb[b][:, i, :], op=ALU.mult,
                 )
@@ -443,8 +455,9 @@ def tile_contextualizer_t_kernel(tc, x, spatial_proj, out):
         s_sumsq(5)
 
         for p in range(-1, NQ + 1):
-            v_mask(2 * p + 2)
-            v_mask(2 * p + 3)
+            if not EARLY(p + 1):
+                v_mask(2 * p + 2)
+                v_mask(2 * p + 3)
             v_quant_xn(p + 2)
             pe_cosim(2 * p + 4)
             pe_cosim(2 * p + 5)
@@ -458,8 +471,9 @@ def tile_contextualizer_t_kernel(tc, x, spatial_proj, out):
                 s_evac(p + 3)
                 if p > 0:
                     s_rsq(p + 5)
-            s_place(2 * p + 2)
-            s_place(2 * p + 3)
+            if not EARLY(p + 1):
+                s_place(2 * p + 2)
+                s_place(2 * p + 3)
             if p >= 0:
                 s_group(p + 2)
                 s_scale(p + 5, SSC(p + 5))
@@ -474,6 +488,10 @@ def tile_contextualizer_t_kernel(tc, x, spatial_proj, out):
                 v_quant_attn(2 * p + 1, 1)
             if p % 2 == 0 and p > 0 and p == NQ - 2:
                 v_quant_x0((p + 1) // 4, ((p + 1) % 4) // 2)
+            if EARLY(p + 2):
+                for t in (2 * p + 4, 2 * p + 5):
+                    v_mask(t)
+                    g_place(t)
             gate(2 * p - 2, False)
             if p >= NQ - 1:
                 store(2 * p - 2, 1)

@@ -32,7 +32,7 @@ def EARLY(p):
 
 
 def SSC(q):
-    return (0,) if q >= 5 and q % 4 == 3 else ()
+    return ()
 
 
 def PLACE(p):
@@ -192,6 +192,11 @@ def tile_contextualizer_t_kernel(tc, x, spatial_proj, out):
             xt = tp.tile([P, 4, P], F32, name="xt")
             chunk[q]["xt"] = xt
             words = xn[:].rearrange("p k d -> p (k d)").bitcast(F32)
+            for k in range(2 if q >= 3 else 0):
+                nc.tensor.matmul(
+                    xt[:].rearrange("p v r -> p (v r)"), lhsT=ident[:], rhs=x0_sb[q // 4][:, 2 * (q % 4), :],
+                    start=True, stop=True,
+                )
             for v in range(4):
                 nc.tensor.transpose(xt[:, v, :], words[:, v * P : (v + 1) * P], ident_f32[:])
 

from contextlib import ExitStack

import concourse.mybir as mybir
from concourse.masks import make_identity

BF16 = mybir.dt.bfloat16
F32 = mybir.dt.float32
U32 = mybir.dt.uint32
U8 = mybir.dt.uint8
I32 = mybir.dt.int32
FP8X4 = mybir.dt.float8_e4m3fn_x4
ACT = mybir.ActivationFunctionType
ALU = mybir.AluOpType

B, N, D = 4, 1024, 512
P = 128
NT = N // P
EPS = 1e-08
FLOPS = 2 * 2 * B * N * N * D

PIN = True
NQ = 4 * B
NS = NT * B


def ASIDE(p):
    return 0 < p < NQ - 1 and p % 4 in (0, 3)


def EARLY(p):
    return p in (4, 8, 12)


def SSC(q):
    return ()


def PLACE(p):
    return False


def tile_contextualizer_t_kernel(tc, x, spatial_proj, out):
    nc = tc.nc
    with ExitStack() as stack:
        const = stack.enter_context(tc.tile_pool(name="const", bufs=1))
        junkp = stack.enter_context(tc.tile_pool(name="junkp", bufs=4))
        small = stack.enter_context(tc.tile_pool(name="small", bufs=2))
        xnp = stack.enter_context(tc.tile_pool(name="xnp", bufs=4))
        gxp = stack.enter_context(tc.tile_pool(name="gxp", bufs=3))
        xqp = stack.enter_context(tc.tile_pool(name="xqp", bufs=2))
        g0p = stack.enter_context(tc.tile_pool(name="g0p", bufs=2))
        x0qp = stack.enter_context(tc.tile_pool(name="x0qp", bufs=2))
        aqp = stack.enter_context(tc.tile_pool(name="aqp", bufs=4))
        outp = stack.enter_context(tc.tile_pool(name="outp", bufs=4))
        tp = stack.enter_context(tc.psum_pool(name="tp", bufs=1))
        ps1 = stack.enter_context(tc.psum_pool(name="ps1", bufs=5))
        ps2 = stack.enter_context(tc.psum_pool(name="ps2", bufs=1))
        dgp = stack.enter_context(tc.tile_pool(name="dgp", bufs=2))
        csp = stack.enter_context(tc.tile_pool(name="csp", bufs=2))
        if PIN:
            stack.enter_context(tc.manual_schedule())

        x0_first = const.tile([P, NT, D], BF16, name="x0_first")
        x1_first = const.tile([P, NT, D], BF16, name="x1_first")
        xs_in = [None] + [const.tile([P, NT, 2 * D], BF16, name="xin%d" % b) for b in range(1, B)]
        x0_sb = [x0_first[:]] + [xs_in[b][:, :, 0:D] for b in range(1, B)]
        x1_sb = [x1_first[:]] + [xs_in[b][:, :, D : 2 * D] for b in range(1, B)]

        def load_x(b, i0, n):
            nc.sync.dma_start(
                out=xs_in[b][:, i0 : i0 + n, :],
                in_=x[b][i0 * P : (i0 + n) * P, :].rearrange("(i p) c -> p i c", p=P),
            )

        spn = const.tile([P, 9 * N], BF16, name="spn")
        spv = spn[:, 0 : NT * N].rearrange("p (i m) -> p i m", m=N)
        spd = spn[:, 0 : NT * (N + P)].rearrange("p (i w) -> p i w", w=N + P)[:, :, 0:P]

        def load_first(dst, i0, n, c0):
            nc.sync.dma_start(
                out=dst[:, i0 : i0 + n, :],
                in_=x[0][i0 * P : (i0 + n) * P, c0 : c0 + D].rearrange("(i p) c -> p i c", p=P),
            )

        load_first(x0_first, 0, 2, 0)
        load_first(x0_first, 2, 2, 0)
        nc.sync.dma_start(
            out=spv[:, 0:4, 0:512],
            in_=spatial_proj[0:512, 0:512].rearrange("(i p) m -> p i m", p=P),
        )
        load_first(x0_first, 4, 4, 0)
        nc.sync.dma_start(
            out=spv[:, 4:8, :],
            in_=spatial_proj[512:1024, :].rearrange("(i p) m -> p i m", p=P),
        )
        load_first(x1_first, 0, 8, D)
        for b in range(1, B):
            load_x(b, 0, 4)
            load_x(b, 4, 4)

        eps = const.tile([P, 1], F32, name="eps")
        nc.vector.memset(eps[:], EPS)
        warm = const.tile([P, 1], F32, name="warm")
        nc.scalar.activation(out=warm[:], in_=eps[:], func=ACT.Abs_reciprocal_sqrt)
        ident = const.tile([P, P], BF16, name="ident")
        ident_f32 = const.tile([P, P], F32, name="ident_f32")
        make_identity(nc, ident_f32[:])
        make_identity(nc, ident[:])
        ga_all = const.tile([P, 2, 12, 4 * P], BF16, name="ga_all", align_bytes=64)
        ga_i32 = (
            ga_all[:].rearrange("p a u c -> p (a u c)").bitcast(I32)
            .rearrange("p (a u w) -> p a u w", a=2, u=12)
        )
        nc.vector.memset(ga_i32[:, :, 0:3, :], 0)
        ga_diag = ga_i32[:, :, 4:12, :].rearrange("p a (i g) w -> p a i g w", g=2)[:, :, 0:3, 1, :]
        nc.vector.memset(ga_diag[:, 0], 0)

        def unit0(i):
            return i if i < 4 else 4 + 2 * (i - 4)

        state = [dict() for b in range(B)]
        chunk = [dict() for q in range(NQ)]
        tl = [dict() for s in range(NS)]

        def s_sumsq(q, fin=True):
            if not 0 <= q < NQ:
                return
            b, c = q // 4, q % 4
            st = state[b]
            if c == 0:
                st["ss"] = small.tile([P, NT], F32, name="ss")
                st["rn"] = small.tile([P, NT], F32, name="rn")
            i0 = 2 * c
            for i in (i0, i0 + 1):
                junk = junkp.tile([P, D], BF16, name="junk")
                if q == 0 and i == 1:
                    nc.vector.scalar_tensor_tensor(
                        out=junk[:], in0=x0_sb[b][:, i, :], scalar=1.0, in1=x0_sb[b][:, i, :],
                        op0=ALU.mult, op1=ALU.mult, accum_out=st["ss"][:, i : i + 1],
                    )
                    continue
                nc.scalar.activation(
                    out=junk[:], in_=x0_sb[b][:, i, :], func=ACT.Square,
                    accum_out=st["ss"][:, i : i + 1],
                )
            if fin:
                s_rsq(q)

        def s_rsq(q):
            if not 0 <= q < NQ:
                return
            st, i0 = state[q // 4], 2 * (q % 4)
            nc.scalar.activation(
                out=st["rn"][:, i0 : i0 + 2], in_=st["ss"][:, i0 : i0 + 2],
                func=ACT.Abs_reciprocal_sqrt, bias=eps[:, 0:1],
            )

        def s_scale(q, ks):
            if not 0 <= q < NQ:
                return
            b, c = q // 4, q % 4
            st = state[b]
            if "xn" not in chunk[q]:
                chunk[q]["xn"] = xnp.tile([P, 2, D], BF16, name="xn")
            xn = chunk[q]["xn"]
            for k in ks:
                i = 2 * c + k
                nc.scalar.activation(
                    out=xn[:, k, :], in_=x0_sb[b][:, i, :],
                    func=ACT.Copy, scale=st["rn"][:, i : i + 1],
                )

        def scale(q, ks=(0, 1)):
            if not 0 <= q < NQ:
                return
            b, c = q // 4, q % 4
            st = state[b]
            if "xn" not in chunk[q]:
                chunk[q]["xn"] = xnp.tile([P, 2, D], BF16, name="xn")
            xn = chunk[q]["xn"]
            for k in ks:
                i = 2 * c + k
                nc.vector.tensor_scalar(
                    out=xn[:, k, :], in0=x0_sb[b][:, i, :],
                    scalar1=st["rn"][:, i : i + 1], scalar2=None, op0=ALU.mult,
                )

        def pe_transpose(q):
            if not 0 <= q < NQ:
                return
            xn = chunk[q]["xn"]
            xt = tp.tile([P, 4, P], F32, name="xt")
            chunk[q]["xt"] = xt
            words = xn[:].rearrange("p k d -> p (k d)").bitcast(F32)
            for k in range(2 if q >= 3 else 0):
                nc.tensor.matmul(
                    xt[:].rearrange("p v r -> p (v r)"), lhsT=ident[:], rhs=x0_sb[q // 4][:, 2 * (q % 4), :],
                    start=True, stop=True,
                )
            for v in range(4):
                nc.tensor.transpose(xt[:, v, :], words[:, v * P : (v + 1) * P], ident_f32[:])

        def s_evac(q):
            if not 0 <= q < NQ:
                return
            gx = gxp.tile([P, 2, P, 4], BF16, name="gx", align_bytes=64)
            chunk[q]["gx"] = gx
            nc.scalar.copy(
                out=gx[:].rearrange("p k r t -> p (k r t)").bitcast(F32)
                .rearrange("p (k r u) -> p k r u", k=2, u=2),
                in_=chunk[q]["xt"][:].rearrange("p (k u) r -> p k r u", u=2),
            )

        def v_quant_xn(q):
            if not 0 <= q < NQ:
                return
            b, c = q // 4, q % 4
            st = state[b]
            if c == 0:
                st["xq"] = xqp.tile([P, N], U32, name="xq", align_bytes=64)
                st["xs"] = xqp.tile([P, N], U8, name="xs", align_bytes=64)
            cols = slice(c * 256, (c + 1) * 256)
            nc.vector.quantize_mx(
                out=st["xq"][:, cols].bitcast(FP8X4), scales=st["xs"][:, cols],
                in_=chunk[q]["gx"][:].rearrange("p k r t -> p (k r t)"),
            )

        def v_regroup(d0, d1):
            st = state[0]
            if d0 == 0:
                st["g0_0"] = g0p.tile([P, D, 4], BF16, name="g0", align_bytes=64)
            nc.vector.tensor_copy(
                out=st["g0_0"][:, d0:d1, :].rearrange("p (c i) t -> p c t i", i=4),
                in_=x0_first[:, 0:4, d0:d1].rearrange("p t (c i) -> p c t i", i=4),
            )

        def s_group(q):
            if not 2 <= q < NQ:
                return
            b, g, h = q // 4, q % 4 // 2, q % 2
            st = state[b]
            if h == 0:
                st["g0_%d" % g] = g0p.tile([P, D, 4], BF16, name="g0", align_bytes=64)
            cols = slice(256 * h, 256 * h + 256)
            dst = st["g0_%d" % g][:, cols, :].rearrange("p (c i) t -> p c t i", i=4)
            src = x0_sb[b][:, 4 * g : 4 * g + 4, cols].rearrange("p t (c i) -> p c t i", i=4)
            if False:
                nc.vector.tensor_copy(out=dst, in_=src)
            else:
                nc.scalar.copy(out=dst, in_=src)

        def v_quant_x0(b, g):
            if not 0 <= b < B:
                return
            st = state[b]
            if g == 0:
                st["x0q"] = x0qp.tile([P, 2, D], U32, name="x0q", align_bytes=64)
                st["x0s"] = x0qp.tile([P, 2, D], U8, name="x0s", align_bytes=64)
            nc.vector.quantize_mx(
                out=st["x0q"][:, g, :].bitcast(FP8X4), scales=st["x0s"][:, g, :],
                in_=st["g0_%d" % g][:].rearrange("p d t -> p (d t)"),
            )

        spg = {}
        pst_t = {}

        def mask_sel(half):
            dia = spd[:, 4 * half : 4 * half + 4, :]
            nc.gpsimd.affine_select(
                out=dia, in_=dia, pattern=[[0, 4], [-1, P]],
                compare_op=ALU.is_ge, fill=0.0, base=0, channel_multiplier=1,
            )

        def mask_t(rows, pool, tag):
            pst = pool.tile([P, 8, P], BF16, name="pst", tag=tag)
            n = 0
            for i in rows:
                pst_t[i] = pst[:, n : n + i + 1, :]
                for j in range(i + 1):
                    nc.tensor.transpose(pst[:, n + j, :], spv[:, i, j * P : (j + 1) * P], ident[:])
                n += i + 1

        def mask_e(i):
            for g in range(i // 4 + 1):
                T = min(i - 4 * g, 3) + 1
                sg = const.tile([P, P, T], BF16, name="spg%d_%d" % (i, g))
                src = pst_t[i][:, 4 * g : 4 * g + T, :].rearrange("p t n -> p n t")
                if i >= 6:
                    nc.scalar.copy(out=sg[:], in_=src)
                else:
                    nc.vector.tensor_copy(out=sg[:], in_=src)
                spg[(i, g)] = sg

        def pe_cosim(s):
            if not 0 <= s < NS:
                return
            b, i = s // NT, s % NT
            xq, xs = state[b]["xq"], state[b]["xs"]
            tl[s]["c1"] = []
            for g in range(i // 4 + 1):
                T = min(i - 4 * g, 3) + 1
                c1 = ps1.tile([P, 4, P], F32, name="c1", tag="c1")
                tl[s]["c1"].append(c1)
                for t in range(T):
                    j = 4 * g + t
                    nc.tensor.matmul_mx(
                        out=c1[:, t, :],
                        lhsT=xq[:, j * P : (j + 1) * P].bitcast(FP8X4),
                        lhsT_scale=xs[:, j * P : (j + 1) * P],
                        rhs=xq[:, i * P : (i + 1) * P].bitcast(FP8X4),
                        rhs_scale=xs[:, i * P : (i + 1) * P],
                        start=True, stop=True,
                    )

        def v_mask(s):
            if not 0 <= s < NS:
                return
            b, i = s // NT, s % NT
            for g in range(i // 4 + 1):
                T = min(i - 4 * g, 3) + 1
                ga = ga_all[:, b % 2, unit0(i) + g, :].rearrange("p (n t) -> p n t", t=4)[:, :, 0:T]
                if T <= 2 and s > 1:
                    tl[s]["place"] = ga
                    ga = dgp.tile([P, P, T], BF16, name="dg%d" % T)
                    tl[s]["dg"] = ga
                nc.vector.tensor_tensor(
                    out=ga[:],
                    in0=tl[s]["c1"][g][:, 0:T, :].rearrange("p t n -> p n t"),
                    in1=spg[(i, g)][:],
                    op=ALU.mult,
                )

        def s_place(s):
            if not 0 <= s < NS or "place" not in tl[s]:
                return
            nc.scalar.copy(out=tl[s]["place"], in_=tl[s]["dg"][:])

        def g_place(s):
            nc.gpsimd.tensor_scalar(
                out=tl[s]["place"], in0=tl[s]["dg"][:], scalar1=1.0, scalar2=0.0, op0=ALU.mult, op1=ALU.add,
            )

        def v_quant_attn(s, n):
            if not 0 <= s < NS:
                return
            b, i = s // NT, s % NT
            u0, nu = unit0(i), n * (i // 4 + 1)
            aq = aqp.tile([P, 4, P], U32, name="aq", align_bytes=64)
            asc = aqp.tile([P, 4, P], U8, name="asc", align_bytes=64)
            for k in range(n):
                tl[s + k]["aq"], tl[s + k]["asc"], tl[s + k]["u"] = aq, asc, k * (i // 4 + 1)
            nc.vector.quantize_mx(
                out=aq[:, 0:nu, :].rearrange("p u n -> p (u n)").bitcast(FP8X4),
                scales=asc[:, 0:nu, :].rearrange("p u n -> p (u n)"),
                in_=ga_all[:, b % 2, u0 : u0 + nu, :].rearrange("p u c -> p (u c)"),
            )

        def pe_ctx(s):
            if not 0 <= s < NS:
                return
            b, i = s // NT, s % NT
            st = state[b]
            ng = i // 4 + 1
            tag = "ctx%d" % (i % 2)
            if s < NS - 4:
                ctxp = ps2.tile([P, D], F32, name="ctxp", tag=tag)
            else:
                ctxp = ps1.tile([P, D], F32, name="ctxl", tag="c1")
            tl[s]["ctx"] = ctxp
            for g in range(ng):
                u = tl[s]["u"] + g
                nc.tensor.matmul_mx(
                    out=ctxp[:],
                    lhsT=tl[s]["aq"][:, u, :].bitcast(FP8X4), lhsT_scale=tl[s]["asc"][:, u, :],
                    rhs=st["x0q"][:, g, :].bitcast(FP8X4), rhs_scale=st["x0s"][:, g, :],
                    start=(g == 0), stop=(g == ng - 1),
                )

        def s_take(s):
            cs = csp.tile([P, D], F32, name="cs")
            tl[s]["cs"] = cs
            nc.scalar.copy(out=cs[:], in_=tl[s]["ctx"][:])

        def gate(s, aside):
            if not 0 <= s < NS:
                return
            b, i = s // NT, s % NT
            st = state[b]
            if "o" not in tl[s]:
                o = outp.tile([P, 2, D], F32, name="o")
                tl[s - s % 2]["o"], tl[s - s % 2 + 1]["o"] = o, o
            o = tl[s]["o"]
            if aside:
                if b == 0:
                    tl[s]["row"] = x1_first[:, i - 2 : i, :].rearrange("p i d -> p (i d)").bitcast(F32)
                else:
                    tl[s]["row"] = xs_in[b][:, i - 1, :].bitcast(F32)
                nc.gpsimd.tensor_tensor(
                    out=tl[s]["row"], in0=tl[s]["cs"][:], in1=x1_sb[b][:, i, :], op=ALU.mult,
                )
            else:
                nc.vector.tensor_tensor(
                    out=o[:, i % 2, :], in0=tl[s]["ctx"][:], in1=x1_sb[b][:, i, :], op=ALU.mult,
                )

        def gate_part(s, c):
            b, i = s // NT, s % NT
            cols = slice(c, c + D // 2)
            o = tl[s]["o"][:, 1, cols]
            nc.vector.tensor_tensor(out=o, in0=tl[s]["ctx"][:, cols], in1=x1_sb[b][:, i, cols], op=ALU.mult)
            nc.sync.dma_start(out=out[b][i * P : (i + 1) * P, cols], in_=o)

        def store(s, n):
            if not 0 <= s < NS:
                return
            b, i = s // NT, s % NT
            if "row" in tl[s]:
                nc.sync.dma_start(out=out[b][i * P : (i + 1) * P, :], in_=tl[s]["row"])
            else:
                nc.sync.dma_start(
                    out=out[b][i * P : (i + n) * P, :].rearrange("(i p) d -> p i d", p=P),
                    in_=tl[s]["o"][:, i % 2 : i % 2 + n, :],
                )

        H2 = D // 2
        s_sumsq(0)
        nc.vector.memset(ga_diag[:, 1], 0)
        scale(0)
        pe_transpose(0)
        s_sumsq(1)
        s_evac(0)
        v_regroup(0, H2)
        mask_sel(0)
        mask_t((0, 1, 2), ps1, "c1")
        scale(1)
        pe_transpose(1)
        mask_sel(1)
        mask_t((3,), ps1, "c1")
        v_regroup(H2, D)
        for i in range(3):
            mask_e(i)
        s_sumsq(2)
        v_quant_xn(0)
        pe_cosim(0)
        pe_cosim(1)
        mask_e(3)
        s_evac(1)
        scale(2)
        v_quant_x0(0, 0)
        pe_transpose(2)
        mask_t((4,), ps1, "c1")
        mask_t((5,), ps1, "c1")
        mask_t((6,), ps1, "c1")
        mask_t((7,), ps2, "ctx1")
        s_sumsq(3)
        s_evac(2)
        mask_e(6)
        s_sumsq(4)
        mask_e(7)
        s_sumsq(5)

        for p in range(-1, NQ + 1):
            if not EARLY(p + 1):
                v_mask(2 * p + 2)
                v_mask(2 * p + 3)
            v_quant_xn(p + 2)
            pe_cosim(2 * p + 4)
            pe_cosim(2 * p + 5)
            if p == -1:
                mask_e(4)
            if p != 0:
                scale(p + 4, [k for k in range(2) if k not in SSC(p + 4)])
            if p == -1:
                mask_e(5)
            if p >= 0:
                s_evac(p + 3)
                if p > 0:
                    s_rsq(p + 5)
            if not EARLY(p + 1):
                s_place(2 * p + 2)
                s_place(2 * p + 3)
            if p >= 0:
                s_group(p + 2)
                s_scale(p + 5, SSC(p + 5))
                s_sumsq(p + 6, False)
            if p != 0:
                pe_transpose(p + 4)
            if p == NQ - 1:
                v_quant_attn(2 * p, 1)
            else:
                v_quant_attn(2 * p, 2)
            if p == NQ - 1:
                v_quant_attn(2 * p + 1, 1)
            if p % 2 == 0 and p > 0 and p == NQ - 2:
                v_quant_x0((p + 1) // 4, ((p + 1) % 4) // 2)
            if EARLY(p + 2):
                for t in (2 * p + 4, 2 * p + 5):
                    v_mask(t)
                    g_place(t)
            gate(2 * p - 2, False)
            if p >= NQ - 1:
                store(2 * p - 2, 1)
            if p == NQ:
                for c in (0, D // 2):
                    gate_part(NS - 1, c)
                break
            if p % 2 == 0 and p > 0:
                gate(2 * p - 1, ASIDE(p - 1))
                if not (p == NQ - 2):
                    v_quant_x0((p + 1) // 4, ((p + 1) % 4) // 2)
                pe_ctx(2 * p)
            else:
                pe_ctx(2 * p)
                gate(2 * p - 1, ASIDE(p - 1))
            pe_ctx(2 * p + 1)
            if ASIDE(p):
                s_take(2 * p + 1)
            if p == NQ - 1:
                store(2 * p - 1, 1)
            elif ASIDE(p - 1):
                store(2 * p - 2, 1)
                store(2 * p - 1, 1)
            else:
                store(2 * p - 2, 2)
            if p == 0:
                scale(p + 4)
                pe_transpose(p + 4)
